import numpy as np
import ml_dtypes


def mxq(x, axis, fmt="e4m3"):
    dtype, down = {"e4m3": (ml_dtypes.float8_e4m3fn, 7), "e5m2": (ml_dtypes.float8_e5m2, 14)}[fmt]
    v = np.moveaxis(np.asarray(x, np.float32).astype(ml_dtypes.bfloat16).astype(np.float64), axis, -1)
    blocks = v.reshape(v.shape[:-1] + (-1, 32))
    amax = np.abs(blocks).max(-1, keepdims=True)
    byte = np.maximum(np.where(amax > 0, np.frexp(amax)[1] - 1 + 127, 0) - down, 1)
    scale = np.exp2(byte - 127.0)
    codes = (blocks / scale).astype(np.float32).astype(dtype).astype(np.float64)
    return np.moveaxis((codes * scale).reshape(v.shape), -1, axis)


WIDE = False


def mx_kscale(k):
    if not WIDE:
        return np.ones(k)
    levels = np.array([10, -10, 5, -5, 0])
    if k % 512:
        return np.exp2(np.random.permutation(np.resize(levels, k // 32))).repeat(32)
    a = np.empty((k // 512, 16))
    for p in range(k // 512):
        a[p, :8] = np.random.permutation(np.resize(levels, 8))
        for g in range(8):
            far = levels[np.abs(levels - a[p, g]) >= 10]
            a[p, g + 8] = far[np.random.randint(len(far))]
    return np.exp2(a.ravel()).repeat(32)


BF16 = ml_dtypes.bfloat16


def bf(x):
    return np.asarray(x, np.float32).astype(BF16)


def f64(x):
    return np.asarray(x).astype(np.float64)


B, S, D_MODEL, N_HEADS, QK_ROPE, QK_NOPE, KV_LORA, V_DIM = 4, 256, 1024, 8, 128, 128, 512, 128
QK_DIM = QK_ROPE + QK_NOPE
ROPE_BASE = 10000.0
T, J = B * S, N_HEADS * QK_DIM


def rope_tables():
    freqs = 1.0 / (ROPE_BASE ** (np.arange(0, QK_ROPE, 2) / QK_ROPE))
    t = np.arange(S)[:, None] * freqs[None, :]
    return np.cos(t)[None, :, None, :], np.sin(t)[None, :, None, :]


def rope_backward(g):
    cos, sin = rope_tables()
    g1 = g[..., 0::2]
    g2 = g[..., 1::2]
    return np.stack([g1 * cos + g2 * sin, g2 * cos - g1 * sin], axis=-1).reshape(g.shape)


def setup_inputs():
    s = mx_kscale(T).reshape(B, S, 1)
    u = np.repeat(mx_kscale(J)[0::2], 2)
    x0 = bf(np.random.standard_normal((B, S, D_MODEL)))
    w0 = bf(np.random.standard_normal((D_MODEL, J)) / np.sqrt(D_MODEL))
    g = np.random.standard_normal((B, S, N_HEADS, QK_DIM)) * np.exp2(np.random.randint(-6, 1, (B, S, 1, 1)))
    return {"x": bf(f64(x0) * s),
            "Wq": bf(f64(w0) / u),
            "grad_out": bf(g / s[..., None] * u.reshape(N_HEADS, QK_DIM))}


def reference(x, Wq, grad_out):
    g = f64(grad_out)
    dq = np.concatenate([g[..., :QK_NOPE], rope_backward(g[..., QK_NOPE:])], axis=-1).reshape(T, J)
    dx = (mxq(dq, 1, "e5m2") @ mxq(f64(Wq), 1, "e4m3").T).reshape(B, S, D_MODEL)
    dw = mxq(f64(x).reshape(T, D_MODEL), 0, "e4m3").T @ mxq(dq, 0, "e5m2")
    return dx, dw

@@ -1,0 +1,400 @@
+import math
+from contextlib import ExitStack
+
+import concourse.mybir as mybir
+from concourse.masks import make_identity
+
+F32 = mybir.dt.float32
+BF16 = mybir.dt.bfloat16
+I32 = mybir.dt.int32
+U32 = mybir.dt.uint32
+U8 = mybir.dt.uint8
+E4M3 = mybir.dt.float8_e4m3fn_x4
+E5M2 = mybir.dt.float8_e5m2_x4
+ADD = mybir.AluOpType.add
+SUB = mybir.AluOpType.subtract
+MULT = mybir.AluOpType.mult
+IS_GE = mybir.AluOpType.is_ge
+SIN = mybir.ActivationFunctionType.Sin
+
+P = 128
+T = 1024
+D = 1024
+J = 2048
+S = 256
+HEAD = 256
+ROPE = 128
+K_PASS = 512
+TG = T // K_PASS
+FC = J // K_PASS
+HPC = K_PASS // HEAD
+ROPE_BASE = 10000.0
+FLOPS = 2 * 2 * T * D * J
+
+
+def tile_multiheadlatentattention_pb_v_kernel(tc, x, wq, grad_out, out_0, out_1):
+    nc = tc.nc
+    x_v = x.rearrange("b s d -> (b s) d").rearrange("(g p j) d -> g p j d", g=TG, j=4)
+    g_v = grad_out.rearrange("b s h q -> (b s) (h q)").rearrange("(g p j) f -> g p j f", g=TG, j=4)
+    w_v = wq.rearrange("(n p) f -> n p f", p=P)
+    o0_v = out_0.rearrange("b s d -> (b s) d").rearrange("(g p j) d -> g p j d", g=TG, j=4)
+    o1_v = out_1.rearrange("(n p) f -> p n f", p=P)
+
+    with ExitStack() as ctx:
+        keep = ctx.enter_context(tc.tile_pool(name="keep", bufs=1))
+        work = ctx.enter_context(tc.tile_pool(name="work", bufs=2))
+        psum = ctx.enter_context(tc.psum_pool(name="psum", bufs=1))
+
+        g_sb = {}
+        x_sb = {}
+        w_sb = {}
+        tok_codes = {}
+        tok_scales = {}
+        feat_codes = {}
+        feat_scales = {}
+        x_codes = {}
+        x_scales = {}
+        w_codes = {}
+        w_scales = {}
+        mul_c = {}
+        mul_s = {}
+        grouped = {}
+        banks = {}
+        w_grp = {}
+
+        turn = {"tr": 0, "acc": 0}
+        ring = {"tr": [0, 1], "acc": [2, 3, 4, 5, 6, 7]}
+
+        def next_bank(kind):
+            b = ring[kind][turn[kind] % len(ring[kind])]
+            turn[kind] += 1
+            return "bank%d" % b
+
+        def tr_bank():
+            b = next_bank("tr")
+            return psum.tile([P, 2, 2, P], F32, name=b, tag=b)
+
+        def acc_bank():
+            b = next_bank("acc")
+            return psum.tile([P, K_PASS], F32, name=b, tag=b)
+
+        def set_ring(kind, ids):
+            ring[kind] = ids
+            turn[kind] = 0
+
+        def load_g(g, c):
+            t = keep.tile([P, 4, K_PASS], BF16, name="g%d%d" % (g, c), align_bytes=64)
+            nc.sync.dma_start(out=t[:], in_=g_v[g][:, :, c * K_PASS : (c + 1) * K_PASS])
+            g_sb[g, c] = t
+
+        def load_x(g):
+            t = keep.tile([P, 4, D], BF16, name="x%d" % g, align_bytes=64)
+            nc.sync.dma_start(out=t[:], in_=x_v[g])
+            x_sb[g] = t
+
+        def load_w(n):
+            t = work.tile([P, J], BF16, name="w%d" % n, tag="w", bufs=5, align_bytes=64)
+            nc.sync.dma_start(out=t[:], in_=w_v[n])
+            w_sb[n] = t
+
+        pos = keep.tile([P, 4], F32, name="pos")
+        wrap = keep.tile([P, 4], F32, name="wrap")
+        freq = keep.tile([P, ROPE // 2], F32, name="freq")
+        turns = keep.tile([P, 2, 4, ROPE // 2], F32, name="turns")
+        whole = keep.tile([P, 2, 4, ROPE // 2], I32, name="whole")
+        cos_t = keep.tile([P, 4, ROPE], F32, name="cos_t")
+        sin_t = keep.tile([P, 4, ROPE], F32, name="sin_t")
+        ident = keep.tile([P, P], F32, name="ident")
+        warm = keep.tile([P, 1], F32, name="warm")
+
+        def tables():
+            nc.vector.memset(warm[:], 0.0)
+            nc.scalar.activation(warm[:], warm[:], SIN)
+            nc.gpsimd.iota(pos[:], pattern=[[1, 4]], base=0, channel_multiplier=4, allow_small_or_imprecise_dtypes=True)
+            make_identity(nc, ident[:])
+            nc.vector.memset(freq[:, 0:1], 1.0)
+            n = 1
+            while n < ROPE // 2:
+                nc.vector.tensor_scalar(out=freq[:, n : 2 * n], in0=freq[:, 0:n], scalar1=ROPE_BASE ** (-2.0 * n / ROPE), scalar2=None, op0=MULT)
+                n *= 2
+            nc.vector.tensor_scalar(out=wrap[:], in0=pos[:], scalar1=float(S), scalar2=-float(S), op0=IS_GE, op1=MULT)
+            nc.vector.tensor_tensor(out=pos[:], in0=pos[:], in1=wrap[:], op=ADD)
+            nc.vector.scalar_tensor_tensor(
+                out=turns[:, 0],
+                in0=pos[:].unsqueeze(2).to_broadcast([P, 4, ROPE // 2]),
+                scalar=1.0 / (2.0 * math.pi),
+                in1=freq[:].unsqueeze(1).to_broadcast([P, 4, ROPE // 2]),
+                op0=MULT,
+                op1=MULT,
+            )
+            nc.vector.tensor_scalar(out=turns[:, 1], in0=turns[:, 0], scalar1=0.25, scalar2=None, op0=ADD)
+            nc.vector.tensor_copy(out=whole[:], in_=turns[:])
+            nc.vector.tensor_tensor(out=turns[:], in0=turns[:], in1=whole[:], op=SUB)
+            two_pi = 2.0 * math.pi
+            half = turns[:].rearrange("p s j i -> p s (j i)")
+            cos_v = cos_t[:].rearrange("p j (i e) -> p (j i) e", e=2)
+            sin_v = sin_t[:].rearrange("p j (i e) -> p (j i) e", e=2)
+            n_pairs = 4 * ROPE // 2
+            nc.scalar.activation(cos_v, half[:, 1].unsqueeze(2).to_broadcast([P, n_pairs, 2]), SIN, scale=two_pi)
+            nc.scalar.activation(sin_v[:, :, 1], half[:, 0], SIN, scale=two_pi)
+            nc.scalar.activation(sin_v[:, :, 0], half[:, 0], SIN, scale=-two_pi)
+
+        def rope_view(t):
+            return t[:].rearrange("p j (h q) -> p j h q", h=HPC)[:, :, :, HEAD - ROPE :]
+
+        def table_view(t):
+            return t[:].unsqueeze(2).to_broadcast([P, 4, HPC, ROPE])
+
+        def rope_sin(g, c):
+            t = work.tile([P, 4, HPC, ROPE], F32, name="ms%d%d" % (g, c), tag="ms", bufs=2)
+            nc.vector.tensor_tensor(out=t[:], in0=rope_view(g_sb[g, c]), in1=table_view(sin_t), op=MULT)
+            mul_s[g, c] = t
+
+        def rope_cos(g, c):
+            t = work.tile([P, 4, HPC, ROPE], F32, name="mc%d%d" % (g, c), tag="mc", bufs=2)
+            nc.vector.tensor_tensor(out=t[:], in0=rope_view(g_sb[g, c]), in1=table_view(cos_t), op=MULT)
+            mul_c[g, c] = t
+
+        def rope_add(g, c):
+            rows = g_sb[g, c][:].rearrange("p j (h q) -> p (j h) q", h=HPC)[:, :, HEAD - ROPE :]
+            nc.vector.tensor_tensor(
+                out=rows.rearrange("p r (i e) -> p r i e", e=2),
+                in0=mul_c[g, c][:].rearrange("p j h (i e) -> p (j h) i e", e=2),
+                in1=mul_s[g, c][:].rearrange("p j h (i e) -> p (j h) i e", e=2)[:, :, :, ::-1],
+                op=ADD,
+            )
+
+        def tok_copy(g, c, eng):
+            t = work.tile([P, K_PASS, 4], BF16, name="tg%d%d" % (g, c), tag="tg", bufs=3, align_bytes=64)
+            src = g_sb[g, c][:].rearrange("p t (c i) -> p c t i", i=4)
+            dst = t[:].rearrange("p (c i) t -> p c t i", i=4)
+            if eng == "V":
+                nc.vector.tensor_copy(out=dst, in_=src)
+            else:
+                nc.scalar.copy(out=dst, in_=src)
+            grouped["t", g, c] = t
+
+        def flat(t):
+            return t[:].rearrange("p a b -> p (a b)")
+
+        def tok_quant(g, c):
+            q = keep.tile([P, K_PASS], U32, name="tq%d%d" % (g, c), tag="tq%d%d" % (g, c % 2 if g else c), align_bytes=64)
+            s = keep.tile([P, K_PASS], U8, name="ts%d%d" % (g, c), tag="ts%d%d" % (g, c % 2 if g else c), align_bytes=64)
+            nc.vector.quantize_mx(out=q[:].bitcast(E5M2), scales=s[:], in_=flat(grouped["t", g, c]))
+            tok_codes[g, c] = q
+            tok_scales[g, c] = s
+
+        def feat_transpose(g, c):
+            words = g_sb[g, c][:].rearrange("p j f -> p (j f)").bitcast(F32)
+            for half in range(2):
+                bank = tr_bank()
+                for jj in range(2):
+                    base = (2 * half + jj) * (K_PASS // 2)
+                    for u in range(2):
+                        nc.tensor.transpose(bank[:, jj, u, :], words[:, base + u : base + K_PASS // 2 : 2], ident[:])
+                banks["f", g, c, half] = bank
+
+        def feat_evac(g, c):
+            t = work.tile([P, K_PASS, 4], BF16, name="fg%d%d" % (g, c), tag="fg", bufs=3, align_bytes=64)
+            words = flat(t).bitcast(F32)
+            for half in range(2):
+                nc.scalar.copy(
+                    out=words[:, half * K_PASS : (half + 1) * K_PASS].rearrange("p (j r u) -> p j r u", j=2, u=2),
+                    in_=banks["f", g, c, half][:].rearrange("p j u r -> p j r u"),
+                )
+            grouped["f", g, c] = t
+
+        def feat_quant(g, c):
+            q = keep.tile([P, K_PASS], U32, name="fq%d%d" % (g, c), tag="fq%d" % c, align_bytes=64)
+            s = keep.tile([P, K_PASS], U8, name="fs%d%d" % (g, c), tag="fs%d" % c, align_bytes=64)
+            nc.vector.quantize_mx(out=q[:].bitcast(E5M2), scales=s[:], in_=flat(grouped["f", g, c]))
+            feat_codes[g, c] = q
+            feat_scales[g, c] = s
+
+        def w_transpose(n):
+            words = w_sb[n][:].bitcast(F32)
+            for half in range(2):
+                bank = tr_bank()
+                for cc in range(2):
+                    base = (2 * half + cc) * (K_PASS // 2)
+                    for u in range(2):
+                        nc.tensor.transpose(bank[:, cc, u, :], words[:, base + u : base + K_PASS // 2 : 2], ident[:])
+                banks["w", n, half] = bank
+
+        def w_evac(n):
+            for half in range(2):
+                if n == 0:
+                    w_grp[half] = keep.tile([P, 2, D, 4], BF16, name="wg%d" % half, align_bytes=64)
+                words = w_grp[half][:].rearrange("p c d t -> p c (d t)").bitcast(F32)
+                nc.scalar.copy(
+                    out=words[:, :, n * 2 * P : (n + 1) * 2 * P].rearrange("p c (r u) -> p c r u", u=2),
+                    in_=banks["w", n, half][:].rearrange("p c u r -> p c r u"),
+                )
+
+        def w_quant(c):
+            q = keep.tile([P, D], U32, name="wq%d" % c, align_bytes=64)
+            s = keep.tile([P, D], U8, name="ws%d" % c, align_bytes=64)
+            src = w_grp[c // 2][:].rearrange("p c d t -> p c (d t)")[:, c % 2]
+            nc.vector.quantize_mx(out=q[:].bitcast(E4M3), scales=s[:], in_=src)
+            w_codes[c] = q
+            w_scales[c] = s
+
+        def x_copy(g, eng):
+            t = work.tile([P, D, 4], BF16, name="xg%d" % g, tag="xg", bufs=1, align_bytes=64)
+            src = x_sb[g][:].rearrange("p t (c i) -> p c t i", i=4)
+            dst = t[:].rearrange("p (c i) t -> p c t i", i=4)
+            if eng == "V":
+                nc.vector.tensor_copy(out=dst, in_=src)
+            else:
+                nc.scalar.copy(out=dst, in_=src)
+            grouped["x", g] = t
+
+        def x_quant(g):
+            q = keep.tile([P, D], U32, name="xq%d" % g, align_bytes=64)
+            s = keep.tile([P, D], U8, name="xs%d" % g, align_bytes=64)
+            nc.vector.quantize_mx(out=q[:].bitcast(E4M3), scales=s[:], in_=flat(grouped["x", g]))
+            x_codes[g] = q
+            x_scales[g] = s
+
+        def evac(eng, dst, bank):
+            if eng == "V":
+                nc.vector.tensor_copy(out=dst, in_=bank[:])
+            else:
+                nc.scalar.copy(out=dst, in_=bank[:])
+
+        def out0_passes(g, j, n, chunks):
+            rows = slice(j * P, (j + 1) * P)
+            cols = slice(n * K_PASS, (n + 1) * K_PASS)
+            if chunks[0] == 0:
+                banks["o", g, j, n] = acc_bank()
+            for c in chunks:
+                nc.tensor.matmul_mx(
+                    out=banks["o", g, j, n][:],
+                    lhsT=feat_codes[g, c][:, rows].bitcast(E5M2),
+                    lhsT_scale=feat_scales[g, c][:, rows],
+                    rhs=w_codes[c][:, cols].bitcast(E4M3),
+                    rhs_scale=w_scales[c][:, cols],
+                    start=(c == 0),
+                    stop=(c == FC - 1),
+                )
+
+        def out0_store(g, j, engs):
+            res = work.tile([P, D], F32, name="res", tag="res", bufs=5)
+            for n in range(2):
+                evac(engs[n], res[:, n * K_PASS : (n + 1) * K_PASS], banks["o", g, j, n])
+            nc.sync.dma_start(out=o0_v[g][:, j, :], in_=res[:])
+
+        def out0(g, j, engs):
+            for n in range(2):
+                out0_passes(g, j, n, range(FC))
+            out0_store(g, j, engs)
+
+        def out1(c, n2, engs):
+            res = work.tile([P, 2, K_PASS], F32, name="res", tag="res", bufs=5)
+            for k in range(2):
+                cols = slice((2 * n2 + k) * P, (2 * n2 + k + 1) * P)
+                acc = acc_bank()
+                for g in range(TG):
+                    nc.tensor.matmul_mx(
+                        out=acc[:],
+                        lhsT=x_codes[g][:, cols].bitcast(E4M3),
+                        lhsT_scale=x_scales[g][:, cols],
+                        rhs=tok_codes[g, c][:].bitcast(E5M2),
+                        rhs_scale=tok_scales[g, c][:],
+                        start=(g == 0),
+                        stop=(g == TG - 1),
+                    )
+                evac(engs[k], res[:, k], acc)
+            nc.sync.dma_start(out=o1_v[:, 2 * n2 : 2 * n2 + 2, c * K_PASS : (c + 1) * K_PASS], in_=res[:])
+
+        load_g(0, 0)
+        load_w(0)
+        load_w(1)
+        load_g(0, 1)
+        load_w(2)
+        load_w(3)
+        load_g(0, 2)
+        tables()
+        rope_sin(0, 0)
+        rope_cos(0, 0)
+        for c in range(FC):
+            if c < FC - 1:
+                rope_sin(0, c + 1)
+            rope_add(0, c)
+            if c < FC - 1:
+                rope_cos(0, c + 1)
+            for n in ((0, 1, 2, 3), (4, 5), (6, 7), ())[c]:
+                w_transpose(n)
+                w_evac(n)
+                if n == 0:
+                    load_w(4)
+                    load_w(5)
+                    load_g(0, 3)
+                if n == 2:
+                    load_w(6)
+                    load_w(7)
+                    load_x(0)
+                    load_g(1, 0)
+                    load_x(1)
+                    load_g(1, 1)
+                    load_g(1, 2)
+                    load_g(1, 3)
+            feat_transpose(0, c)
+            feat_evac(0, c)
+            if c > 0:
+                feat_quant(0, c - 1)
+        x_copy(0, "S")
+        for c in range(FC):
+            w_quant(c)
+            if c == 1:
+                feat_quant(0, FC - 1)
+        tok_copy(0, 0, "V")
+        rope_sin(1, 0)
+        x_quant(0)
+        rope_cos(1, 0)
+        tok_quant(0, 0)
+        for j in range(4):
+            out0(0, j, "SS")
+            if j == 1:
+                x_copy(1, "S")
+        for c in range(FC):
+            if c < FC - 1:
+                rope_sin(1, c + 1)
+            rope_add(1, c)
+            if c == 0:
+                x_quant(1)
+            if c < FC - 1:
+                rope_cos(1, c + 1)
+            feat_transpose(1, c)
+            feat_evac(1, c)
+            if c == 0:
+                tok_copy(0, 1, "S")
+            tok_copy(1, c, "V")
+            if c < FC - 1:
+                tok_quant(0, c + 1)
+                feat_quant(1, c)
+            tok_quant(1, c)
+            if c == FC - 1:
+                feat_quant(1, c)
+            if c == FC - 1:
+                set_ring("acc", [2, 3, 0, 1])
+            for n2 in range(4):
+                out1(c, n2, "SS" if c < FC - 1 else "SV")
+                if n2 == 1 and c < FC - 2:
+                    tok_copy(0, c + 2, "S")
+            if c == 1:
+                set_ring("acc", [4, 5, 6, 7])
+                for j, n in ((0, 0), (0, 1), (1, 0), (1, 1)):
+                    out0_passes(1, j, n, (0, 1))
+                set_ring("acc", [2, 3])
+            if c == 2:
+                for j, n in ((0, 0), (0, 1), (1, 0), (1, 1)):
+                    out0_passes(1, j, n, (2,))
+        set_ring("acc", [2, 3, 0, 1, 4, 5, 6, 7])
+        for j in range(4):
+            if j < 2:
+                for n in range(2):
+                    out0_passes(1, j, n, (3,))
+                out0_store(1, j, "SV")
+            else:
+                out0(1, j, "SV")

@@ -29,6 +29,47 @@ TG = T // K_PASS
 FC = J // K_PASS
 HPC = K_PASS // HEAD
 ROPE_BASE = 10000.0
+TGB = 4
+XM = False
+B4 = False
+FGB = 4
+RESB = 5
+WB = 4
+ORDER = (
+    "TAB::V:9 Lg:00:D:9 Lx:00:D:9 Lw:6:D:9 TN:00:V:9 Lg:01:D:9 XC:00:S:9 QC:00:V:9 Lw:4:D:9 WT:61:D:0 "
+    "QS:00:V:9 WT:60:D:1 Lw:3:D:9 QS:01:V:9 TN:01:S:9 Lg:02:D:9 WT:40:D:2 A:00:V:9 WE:61:S:9 WT:41:D:3 "
+    "Lw:0:D:9 WE:40:S:9 QC:01:V:9 FT:000:D:4 WE:41:S:9 Lw:2:D:9 WT:31:D:5 FE:000:S:9 QS:02:V:9 FT:001:D:6 "
+    "WE:60:S:9 Lw:1:D:9 WT:30:D:7 FE:001:S:9 QC:02:V:9 WT:01:D:0 Lg:03:D:9 WE:30:S:9 WT:00:D:2 WE:31:S:9 "
+    "A:01:V:9 WT:21:D:3 Lw:5:D:9 TR:00:S:9 WT:20:D:4 A:02:V:9 WT:11:D:1 Lw:7:D:9 FT:011:D:6 WE:20:S:9 "
+    "QS:03:V:9 FT:020:D:7 WE:01:S:9 Lg:13:D:9 WT:10:D:5 FE:011:S:9 QC:03:V:9 FT:010:D:4 WE:21:S:9 Lg:10:D:9 "
+    "WT:50:D:0 TR:01:S:9 FQ:00:V:9 WT:70:D:6 Lx:10:D:9 XQ:00:V:9 WT:51:D:3 WE:10:S:9 A:03:V:9 WE:50:S:9 "
+    "Lx:11:D:9 FT:021:D:5 WE:70:S:9 WT:71:D:0 QC:10:V:9 WE:00:S:9 Lg:12:D:9 FT:031:D:6 FE:021:S:9 FT:030:D:2 "
+    "WQ:0:V:9 FE:010:S:9 Lx:01:D:9 WE:71:S:9 FQ:01:V:9 O:0010:D:5 WE:11:S:9 Lg:11:D:9 O:0310:D:4 WQ:1:V:9 "
+    "O:0110:D:0 WE:51:S:9 O:0000:D:1 FE:020:S:9 O:0210:D:3 WQ:2:V:9 FE:031:S:9 O:0300:D:7 FE:030:S:9 "
+    "O:0100:D:6 WQ:3:V:9 O:0301:D:9 XC:10:S:9 O:0111:D:9 O:0200:D:2 O:0311:D:9 O:0201:D:9 FQ:02:V:9 O:0011:D:9 "
+    "O:0211:D:9 FQ:03:V:9 O:0302:D:9 O:0001:D:9 QS:10:V:9 O:0303:D:9 XC:01:S:9 O:0312:D:9 O:0202:D:9 "
+    "O:0101:D:9 XQ:10:V:9 O:0203:D:9 O:0212:D:9 QS:11:V:9 O:0102:D:9 O:0213:D:9 O:0103:D:9 O:0002:D:9 "
+    "QC:11:V:9 XC:11:S:9 O:0313:D:9 O:0012:D:9 O:0112:D:9 O:0113:D:9 TN:10:V:9 O:0013:D:9 A:10:V:9 OE:011:S:9 "
+    "A:11:V:9 OE:020:S:9 FT:101:D:0 OE:021:S:9 TR:10:V:9 FT:100:D:2 OE:001:S:9 ZO:02:D:9 FT:111:D:3 TQ:00:V:9 "
+    "OE:010:S:9 FT:110:D:5 TQ:10:V:9 FE:111:S:9 ZO:01:D:9 O:0003:D:9 XQ:01:V:9 FE:101:S:9 P:01:D:6 XQ:11:V:9 "
+    "OE:031:S:9 P:03:D:3 OE:030:V:9 FE:100:S:9 P:02:D:0 TN:11:V:9 TR:11:S:9 P:05:D:4 ZO:03:D:9 P:00:D:7 "
+    "OE:000:V:9 P:07:D:2 TQ:01:V:9 PE:00:S:9 ZO:00:D:9 P:06:D:1 TQ:11:V:9 FE:110:S:9 P:04:D:7 FQ:10:V:9 "
+    "PE:07:S:9 P:10:D:5 FQ:11:V:9 PE:06:S:9 P:11:D:2 QS:12:V:9 PE:01:S:9 ZP:03:D:9 P:13:D:1 PE:10:S:9 "
+    "O:1300:D:6 QC:13:V:9 PE:11:S:9 O:1301:D:9 ZP:00:D:9 P:15:D:5 PE:02:S:9 P:12:D:2 QC:12:V:9 PE:03:S:9 "
+    "ZP:10:D:9 O:1210:D:0 PE:04:S:9 O:1211:D:9 P:17:D:3 QS:13:V:9 PE:15:S:9 ZP:01:D:9 O:1200:D:7 PE:05:S:9 "
+    "O:1201:D:9 P:14:D:5 A:12:V:9 PE:13:S:9 ZP:02:D:9 O:1000:D:4 PE:14:S:9 O:1001:D:9 P:16:D:1 A:13:V:9 "
+    "PE:12:S:9 ZP:12:D:9 FT:121:D:5 PE:17:S:9 TN:12:V:9 FT:120:D:2 FE:121:S:9 ZP:11:D:9 FT:130:D:3 TN:02:V:9 "
+    "FE:120:S:9 FT:131:D:5 FE:130:S:9 FQ:12:V:9 O:1310:D:2 FE:131:S:9 O:1311:D:9 TR:02:V:9 O:1010:D:3 "
+    "TR:12:S:9 O:1312:D:9 FQ:13:V:9 O:1011:D:9 O:1002:D:9 TQ:02:V:9 O:1302:D:9 O:1202:D:9 TR:03:S:9 PE:16:V:9 "
+    "O:1203:D:9 O:1212:D:9 TQ:12:V:9 O:1303:D:9 ZP:13:D:9 O:1313:D:9 OE:130:S:9 O:1012:D:9 OE:131:V:9 "
+    "O:1213:D:9 TN:13:S:9 O:1003:D:9 OE:120:V:9 P:23:D:5 ZO:13:D:9 OE:121:V:9 P:22:D:1 PE:23:S:9 OE:100:V:9 "
+    "O:1013:D:9 ZO:12:D:9 P:27:D:6 TN:03:S:9 PE:22:V:9 P:26:D:2 TR:13:V:9 ZP:21:D:9 P:24:D:7 OE:101:V:9 "
+    "PE:27:S:9 P:21:D:0 TQ:13:V:9 PE:26:S:9 ZO:10:D:9 P:25:D:5 PE:24:S:9 TQ:03:V:9 P:20:D:4 PE:21:S:9 "
+    "ZP:23:D:9 P:33:D:1 PE:20:V:9 P:31:D:3 PE:25:V:9 ZP:20:D:9 P:32:D:6 P:34:D:2 PE:32:S:9 ZP:22:D:9 P:37:D:7 "
+    "PE:33:S:9 P:30:D:0 PE:31:S:9 ZP:31:D:9 O:1100:D:4 PE:30:V:9 PE:37:S:9 P:35:D:5 PE:34:S:9 O:1110:D:6 "
+    "ZP:30:D:9 O:1101:D:9 PE:35:S:9 P:36:D:1 O:1102:D:9 ZP:32:D:9 PE:36:S:9 O:1103:D:9 O:1111:D:9 OE:110:S:9 "
+    "O:1112:D:9 O:1113:D:9 ZP:33:D:9 OE:111:V:9 ZO:11:D:9 "
+)
 FLOPS = 2 * 2 * T * D * J
 
 
@@ -61,83 +102,85 @@ def tile_multiheadlatentattention_pb_v_kernel(tc, x, wq, grad_out, out_0, out_1)
         grouped = {}
         banks = {}
         w_grp = {}
+        results = {}
 
-        turn = {"tr": 0, "acc": 0}
-        ring = {"tr": [0, 1], "acc": [2, 3, 4, 5, 6, 7]}
+        def tr_bank(b):
+            return psum.tile([P, 2, 2, P], F32, name="bank%d" % b, tag="bank%d" % b)
 
-        def next_bank(kind):
-            b = ring[kind][turn[kind] % len(ring[kind])]
-            turn[kind] += 1
-            return "bank%d" % b
+        def acc_bank(b):
+            return psum.tile([P, K_PASS], F32, name="bank%d" % b, tag="bank%d" % b)
 
-        def tr_bank():
-            b = next_bank("tr")
-            return psum.tile([P, 2, 2, P], F32, name=b, tag=b)
+        def copy(eng, dst, src):
+            if eng == "V":
+                nc.vector.tensor_copy(out=dst, in_=src)
+            else:
+                nc.scalar.copy(out=dst, in_=src)
 
-        def acc_bank():
-            b = next_bank("acc")
-            return psum.tile([P, K_PASS], F32, name=b, tag=b)
-
-        def set_ring(kind, ids):
-            ring[kind] = ids
-            turn[kind] = 0
+        def interleave(eng, dst, src):
+            if B4:
+                for h in range(HPC):
+                    copy(eng, dst[:, h].rearrange("p (k i) j -> p k j i", i=4), src[:, h].rearrange("p (k i) j -> p k j i", i=4))
+            else:
+                copy(eng, dst, src)
 
         def load_g(g, c):
             t = keep.tile([P, 4, K_PASS], BF16, name="g%d%d" % (g, c), align_bytes=64)
             nc.sync.dma_start(out=t[:], in_=g_v[g][:, :, c * K_PASS : (c + 1) * K_PASS])
             g_sb[g, c] = t
 
-        def load_x(g):
-            t = keep.tile([P, 4, D], BF16, name="x%d" % g, align_bytes=64)
-            nc.sync.dma_start(out=t[:], in_=x_v[g])
-            x_sb[g] = t
+        def load_x(g, h):
+            t = keep.tile([P, 4, K_PASS], BF16, name="x%d%d" % (g, h), tag="x", bufs=3, align_bytes=64)
+            nc.sync.dma_start(out=t[:], in_=x_v[g][:, :, h * K_PASS : (h + 1) * K_PASS])
+            x_sb[g, h] = t
 
         def load_w(n):
-            t = work.tile([P, J], BF16, name="w%d" % n, tag="w", bufs=5, align_bytes=64)
+            t = work.tile([P, J], BF16, name="w%d" % n, tag="w", bufs=WB, align_bytes=64)
             nc.sync.dma_start(out=t[:], in_=w_v[n])
             w_sb[n] = t
 
+        HALF = ROPE // 2
         pos = keep.tile([P, 4], F32, name="pos")
-        wrap = keep.tile([P, 4], F32, name="wrap")
-        freq = keep.tile([P, ROPE // 2], F32, name="freq")
-        turns = keep.tile([P, 2, 4, ROPE // 2], F32, name="turns")
-        whole = keep.tile([P, 2, 4, ROPE // 2], I32, name="whole")
+        freq = keep.tile([P, HALF], F32, name="freq")
+        turns = keep.tile([P, 2, 4 * HALF], F32, name="turns")
+        whole = keep.tile([P, 2, 4 * HALF], I32, name="whole")
         cos_t = keep.tile([P, 4, ROPE], F32, name="cos_t")
         sin_t = keep.tile([P, 4, ROPE], F32, name="sin_t")
         ident = keep.tile([P, P], F32, name="ident")
+        ident_b = keep.tile([P, P], BF16, name="ident_b")
         warm = keep.tile([P, 1], F32, name="warm")
 
         def tables():
+            nc.vector.memset(freq[:, 0:1], 1.0)
             nc.vector.memset(warm[:], 0.0)
             nc.scalar.activation(warm[:], warm[:], SIN)
-            nc.gpsimd.iota(pos[:], pattern=[[1, 4]], base=0, channel_multiplier=4, allow_small_or_imprecise_dtypes=True)
+            for q in range(2):
+                nc.gpsimd.iota(pos[q * 64 : (q + 1) * 64, :], pattern=[[1, 4]], base=0, channel_multiplier=4, allow_small_or_imprecise_dtypes=True)
             make_identity(nc, ident[:])
-            nc.vector.memset(freq[:, 0:1], 1.0)
+            if XM:
+                make_identity(nc, ident_b[:])
             n = 1
-            while n < ROPE // 2:
+            while n < HALF:
                 nc.vector.tensor_scalar(out=freq[:, n : 2 * n], in0=freq[:, 0:n], scalar1=ROPE_BASE ** (-2.0 * n / ROPE), scalar2=None, op0=MULT)
                 n *= 2
-            nc.vector.tensor_scalar(out=wrap[:], in0=pos[:], scalar1=float(S), scalar2=-float(S), op0=IS_GE, op1=MULT)
-            nc.vector.tensor_tensor(out=pos[:], in0=pos[:], in1=wrap[:], op=ADD)
             nc.vector.scalar_tensor_tensor(
-                out=turns[:, 0],
-                in0=pos[:].unsqueeze(2).to_broadcast([P, 4, ROPE // 2]),
+                out=turns[:, 0].rearrange("p (j i) -> p j i", j=4),
+                in0=pos[:].unsqueeze(2).to_broadcast([P, 4, HALF]),
                 scalar=1.0 / (2.0 * math.pi),
-                in1=freq[:].unsqueeze(1).to_broadcast([P, 4, ROPE // 2]),
+                in1=freq[:].unsqueeze(1).to_broadcast([P, 4, HALF]),
                 op0=MULT,
                 op1=MULT,
             )
+            nc.vector.tensor_copy(out=whole[:, 0], in_=turns[:, 0])
             nc.vector.tensor_scalar(out=turns[:, 1], in0=turns[:, 0], scalar1=0.25, scalar2=None, op0=ADD)
-            nc.vector.tensor_copy(out=whole[:], in_=turns[:])
-            nc.vector.tensor_tensor(out=turns[:], in0=turns[:], in1=whole[:], op=SUB)
+            nc.vector.tensor_tensor(out=turns[:, 0], in0=turns[:, 0], in1=whole[:, 0], op=SUB)
+            nc.vector.tensor_copy(out=whole[:, 1], in_=turns[:, 1])
             two_pi = 2.0 * math.pi
-            half = turns[:].rearrange("p s j i -> p s (j i)")
             cos_v = cos_t[:].rearrange("p j (i e) -> p (j i) e", e=2)
             sin_v = sin_t[:].rearrange("p j (i e) -> p (j i) e", e=2)
-            n_pairs = 4 * ROPE // 2
-            nc.scalar.activation(cos_v, half[:, 1].unsqueeze(2).to_broadcast([P, n_pairs, 2]), SIN, scale=two_pi)
-            nc.scalar.activation(sin_v[:, :, 1], half[:, 0], SIN, scale=two_pi)
-            nc.scalar.activation(sin_v[:, :, 0], half[:, 0], SIN, scale=-two_pi)
+            nc.scalar.activation(sin_v[:, :, 1], turns[:, 0], SIN, scale=two_pi)
+            nc.scalar.activation(sin_v[:, :, 0], turns[:, 0], SIN, scale=-two_pi)
+            nc.vector.tensor_tensor(out=turns[:, 1], in0=turns[:, 1], in1=whole[:, 1], op=SUB)
+            nc.scalar.activation(cos_v, turns[:, 1].unsqueeze(2).to_broadcast([P, 4 * HALF, 2]), SIN, scale=two_pi)
 
         def rope_view(t):
             return t[:].rearrange("p j (h q) -> p j h q", h=HPC)[:, :, :, HEAD - ROPE :]
@@ -164,15 +207,12 @@ def tile_multiheadlatentattention_pb_v_kernel(tc, x, wq, grad_out, out_0, out_1)
                 op=ADD,
             )
 
-        def tok_copy(g, c, eng):
-            t = work.tile([P, K_PASS, 4], BF16, name="tg%d%d" % (g, c), tag="tg", bufs=3, align_bytes=64)
-            src = g_sb[g, c][:].rearrange("p t (c i) -> p c t i", i=4)
-            dst = t[:].rearrange("p (c i) t -> p c t i", i=4)
-            if eng == "V":
-                nc.vector.tensor_copy(out=dst, in_=src)
-            else:
-                nc.scalar.copy(out=dst, in_=src)
-            grouped["t", g, c] = t
+        def tok_copy(g, c, half, eng):
+            if ("t", g, c) not in grouped:
+                grouped["t", g, c] = work.tile([P, K_PASS, 4], BF16, name="tg%d%d" % (g, c), tag="tg", bufs=TGB, align_bytes=64)
+            src = g_sb[g, c][:].rearrange("p j (h q) -> p h q j", h=HPC)[:, :, half * ROPE : (half + 1) * ROPE, :]
+            dst = grouped["t", g, c][:].rearrange("p (h q) j -> p h q j", h=HPC)[:, :, half * ROPE : (half + 1) * ROPE, :]
+            interleave(eng, dst, src)
 
         def flat(t):
             return t[:].rearrange("p a b -> p (a b)")
@@ -184,52 +224,50 @@ def tile_multiheadlatentattention_pb_v_kernel(tc, x, wq, grad_out, out_0, out_1)
             tok_codes[g, c] = q
             tok_scales[g, c] = s
 
-        def feat_transpose(g, c):
+        def feat_transpose(g, c, half, b):
             words = g_sb[g, c][:].rearrange("p j f -> p (j f)").bitcast(F32)
-            for half in range(2):
-                bank = tr_bank()
-                for jj in range(2):
-                    base = (2 * half + jj) * (K_PASS // 2)
-                    for u in range(2):
-                        nc.tensor.transpose(bank[:, jj, u, :], words[:, base + u : base + K_PASS // 2 : 2], ident[:])
-                banks["f", g, c, half] = bank
+            bank = tr_bank(b)
+            for jj in range(2):
+                base = (2 * half + jj) * (K_PASS // 2)
+                for u in range(2):
+                    nc.tensor.transpose(bank[:, jj, u, :], words[:, base + u : base + K_PASS // 2 : 2], ident[:])
+            banks["f", g, c, half] = bank
 
-        def feat_evac(g, c):
-            t = work.tile([P, K_PASS, 4], BF16, name="fg%d%d" % (g, c), tag="fg", bufs=3, align_bytes=64)
-            words = flat(t).bitcast(F32)
-            for half in range(2):
-                nc.scalar.copy(
-                    out=words[:, half * K_PASS : (half + 1) * K_PASS].rearrange("p (j r u) -> p j r u", j=2, u=2),
-                    in_=banks["f", g, c, half][:].rearrange("p j u r -> p j r u"),
-                )
-            grouped["f", g, c] = t
+        def feat_evac(g, c, half, eng):
+            if ("f", g, c) not in grouped:
+                grouped["f", g, c] = work.tile([P, K_PASS, 4], BF16, name="fg%d%d" % (g, c), tag="fg", bufs=FGB, align_bytes=64)
+            words = flat(grouped["f", g, c]).bitcast(F32)
+            copy(
+                eng,
+                words[:, half * K_PASS : (half + 1) * K_PASS].rearrange("p (j r u) -> p j r u", j=2, u=2),
+                banks["f", g, c, half][:].rearrange("p j u r -> p j r u"),
+            )
 
         def feat_quant(g, c):
-            q = keep.tile([P, K_PASS], U32, name="fq%d%d" % (g, c), tag="fq%d" % c, align_bytes=64)
-            s = keep.tile([P, K_PASS], U8, name="fs%d%d" % (g, c), tag="fs%d" % c, align_bytes=64)
+            q = keep.tile([P, K_PASS], U32, name="fq%d%d" % (g, c), tag="fq%d" % (c if g == 0 or c > 1 else c + 4), align_bytes=64)
+            s = keep.tile([P, K_PASS], U8, name="fs%d%d" % (g, c), tag="fs%d" % (c if g == 0 or c > 1 else c + 4), align_bytes=64)
             nc.vector.quantize_mx(out=q[:].bitcast(E5M2), scales=s[:], in_=flat(grouped["f", g, c]))
             feat_codes[g, c] = q
             feat_scales[g, c] = s
 
-        def w_transpose(n):
+        def w_transpose(n, half, b):
             words = w_sb[n][:].bitcast(F32)
-            for half in range(2):
-                bank = tr_bank()
-                for cc in range(2):
-                    base = (2 * half + cc) * (K_PASS // 2)
-                    for u in range(2):
-                        nc.tensor.transpose(bank[:, cc, u, :], words[:, base + u : base + K_PASS // 2 : 2], ident[:])
-                banks["w", n, half] = bank
+            bank = tr_bank(b)
+            for cc in range(2):
+                base = (2 * half + cc) * (K_PASS // 2)
+                for u in range(2):
+                    nc.tensor.transpose(bank[:, cc, u, :], words[:, base + u : base + K_PASS // 2 : 2], ident[:])
+            banks["w", n, half] = bank
 
-        def w_evac(n):
-            for half in range(2):
-                if n == 0:
-                    w_grp[half] = keep.tile([P, 2, D, 4], BF16, name="wg%d" % half, align_bytes=64)
-                words = w_grp[half][:].rearrange("p c d t -> p c (d t)").bitcast(F32)
-                nc.scalar.copy(
-                    out=words[:, :, n * 2 * P : (n + 1) * 2 * P].rearrange("p c (r u) -> p c r u", u=2),
-                    in_=banks["w", n, half][:].rearrange("p c u r -> p c r u"),
-                )
+        def w_evac(n, half, eng):
+            if half not in w_grp:
+                w_grp[half] = keep.tile([P, 2, D, 4], BF16, name="wg%d" % half, align_bytes=64)
+            words = w_grp[half][:].rearrange("p c d t -> p c (d t)").bitcast(F32)
+            copy(
+                eng,
+                words[:, :, n * 2 * P : (n + 1) * 2 * P].rearrange("p c (r u) -> p c r u", u=2),
+                banks["w", n, half][:].rearrange("p c u r -> p c r u"),
+            )
 
         def w_quant(c):
             q = keep.tile([P, D], U32, name="wq%d" % c, align_bytes=64)
@@ -239,162 +277,131 @@ def tile_multiheadlatentattention_pb_v_kernel(tc, x, wq, grad_out, out_0, out_1)
             w_codes[c] = q
             w_scales[c] = s
 
-        def x_copy(g, eng):
-            t = work.tile([P, D, 4], BF16, name="xg%d" % g, tag="xg", bufs=1, align_bytes=64)
-            src = x_sb[g][:].rearrange("p t (c i) -> p c t i", i=4)
-            dst = t[:].rearrange("p (c i) t -> p c t i", i=4)
-            if eng == "V":
-                nc.vector.tensor_copy(out=dst, in_=src)
-            else:
-                nc.scalar.copy(out=dst, in_=src)
-            grouped["x", g] = t
+        def x_copy(g, h, eng):
+            t = work.tile([P, K_PASS, 4], BF16, name="xg%d%d" % (g, h), tag="xg", bufs=2, align_bytes=64)
+            interleave(eng, t[:].rearrange("p (h d) j -> p h d j", h=HPC), x_sb[g, h][:].rearrange("p j (h d) -> p h d j", h=HPC))
+            grouped["x", g, h] = t
 
-        def x_quant(g):
-            q = keep.tile([P, D], U32, name="xq%d" % g, align_bytes=64)
-            s = keep.tile([P, D], U8, name="xs%d" % g, align_bytes=64)
-            nc.vector.quantize_mx(out=q[:].bitcast(E4M3), scales=s[:], in_=flat(grouped["x", g]))
-            x_codes[g] = q
-            x_scales[g] = s
+        def x_move(g, h, k, b):
+            bank = psum.tile([P, 2, K_PASS], BF16, name="bank%d" % b, tag="bank%d" % b)
+            for q in range(2):
+                cols = slice((2 * k + q) * P, (2 * k + q + 1) * P)
+                nc.tensor.matmul(bank[:, q, :], lhsT=ident_b[:], rhs=x_sb[g, h][:, :, cols].rearrange("p j d -> p d j"), start=True, stop=True)
+            banks["x", g, h, k] = bank
 
-        def evac(eng, dst, bank):
-            if eng == "V":
-                nc.vector.tensor_copy(out=dst, in_=bank[:])
-            else:
-                nc.scalar.copy(out=dst, in_=bank[:])
+        def x_evac(g, h, k, eng):
+            if ("x", g, h) not in grouped:
+                grouped["x", g, h] = work.tile([P, K_PASS, 4], BF16, name="xg%d%d" % (g, h), tag="xg", bufs=2, align_bytes=64)
+            copy(eng, flat(grouped["x", g, h])[:, k * 1024 : (k + 1) * 1024], banks["x", g, h, k][:].rearrange("p a b -> p (a b)"))
 
-        def out0_passes(g, j, n, chunks):
+        def x_quant(g, h):
+            q = keep.tile([P, K_PASS], U32, name="xq%d%d" % (g, h), align_bytes=64)
+            s = keep.tile([P, K_PASS], U8, name="xs%d%d" % (g, h), align_bytes=64)
+            nc.vector.quantize_mx(out=q[:].bitcast(E4M3), scales=s[:], in_=flat(grouped["x", g, h]))
+            x_codes[g, h] = q
+            x_scales[g, h] = s
+
+        def out0_pass(g, j, n, c, b):
             rows = slice(j * P, (j + 1) * P)
             cols = slice(n * K_PASS, (n + 1) * K_PASS)
-            if chunks[0] == 0:
-                banks["o", g, j, n] = acc_bank()
-            for c in chunks:
+            if c == 0:
+                banks["o", g, j, n] = acc_bank(b)
+            nc.tensor.matmul_mx(
+                out=banks["o", g, j, n][:],
+                lhsT=feat_codes[g, c][:, rows].bitcast(E5M2),
+                lhsT_scale=feat_scales[g, c][:, rows],
+                rhs=w_codes[c][:, cols].bitcast(E4M3),
+                rhs_scale=w_scales[c][:, cols],
+                start=(c == 0),
+                stop=(c == FC - 1),
+            )
+
+        def result(key):
+            if key not in results:
+                results[key] = work.tile([P, 2, K_PASS], F32, name="res", tag="res", bufs=RESB)
+            return results[key]
+
+        def out0_evac(g, j, n, eng):
+            copy(eng, result(("o", g, j))[:, n], banks["o", g, j, n][:])
+
+        def out0_store(g, j):
+            nc.sync.dma_start(out=o0_v[g][:, j, :], in_=result(("o", g, j))[:].rearrange("p n d -> p (n d)"))
+
+        def out1_group(c, dt, b):
+            acc = acc_bank(b)
+            cols = slice(dt % 4 * P, (dt % 4 + 1) * P)
+            for g in range(TG):
                 nc.tensor.matmul_mx(
-                    out=banks["o", g, j, n][:],
-                    lhsT=feat_codes[g, c][:, rows].bitcast(E5M2),
-                    lhsT_scale=feat_scales[g, c][:, rows],
-                    rhs=w_codes[c][:, cols].bitcast(E4M3),
-                    rhs_scale=w_scales[c][:, cols],
-                    start=(c == 0),
-                    stop=(c == FC - 1),
+                    out=acc[:],
+                    lhsT=x_codes[g, dt // 4][:, cols].bitcast(E4M3),
+                    lhsT_scale=x_scales[g, dt // 4][:, cols],
+                    rhs=tok_codes[g, c][:].bitcast(E5M2),
+                    rhs_scale=tok_scales[g, c][:],
+                    start=(g == 0),
+                    stop=(g == TG - 1),
                 )
+            banks["p", c, dt] = acc
 
-        def out0_store(g, j, engs):
-            res = work.tile([P, D], F32, name="res", tag="res", bufs=5)
-            for n in range(2):
-                evac(engs[n], res[:, n * K_PASS : (n + 1) * K_PASS], banks["o", g, j, n])
-            nc.sync.dma_start(out=o0_v[g][:, j, :], in_=res[:])
+        def out1_evac(c, dt, eng):
+            copy(eng, result(("p", c, dt // 2))[:, dt % 2], banks["p", c, dt][:])
 
-        def out0(g, j, engs):
-            for n in range(2):
-                out0_passes(g, j, n, range(FC))
-            out0_store(g, j, engs)
+        def out1_store(c, k):
+            nc.sync.dma_start(out=o1_v[:, 2 * k : 2 * k + 2, c * K_PASS : (c + 1) * K_PASS], in_=result(("p", c, k))[:])
 
-        def out1(c, n2, engs):
-            res = work.tile([P, 2, K_PASS], F32, name="res", tag="res", bufs=5)
-            for k in range(2):
-                cols = slice((2 * n2 + k) * P, (2 * n2 + k + 1) * P)
-                acc = acc_bank()
-                for g in range(TG):
-                    nc.tensor.matmul_mx(
-                        out=acc[:],
-                        lhsT=x_codes[g][:, cols].bitcast(E4M3),
-                        lhsT_scale=x_scales[g][:, cols],
-                        rhs=tok_codes[g, c][:].bitcast(E5M2),
-                        rhs_scale=tok_scales[g, c][:],
-                        start=(g == 0),
-                        stop=(g == TG - 1),
-                    )
-                evac(engs[k], res[:, k], acc)
-            nc.sync.dma_start(out=o1_v[:, 2 * n2 : 2 * n2 + 2, c * K_PASS : (c + 1) * K_PASS], in_=res[:])
-
-        load_g(0, 0)
-        load_w(0)
-        load_w(1)
-        load_g(0, 1)
-        load_w(2)
-        load_w(3)
-        load_g(0, 2)
-        tables()
-        rope_sin(0, 0)
-        rope_cos(0, 0)
-        for c in range(FC):
-            if c < FC - 1:
-                rope_sin(0, c + 1)
-            rope_add(0, c)
-            if c < FC - 1:
-                rope_cos(0, c + 1)
-            for n in ((0, 1, 2, 3), (4, 5), (6, 7), ())[c]:
-                w_transpose(n)
-                w_evac(n)
-                if n == 0:
-                    load_w(4)
-                    load_w(5)
-                    load_g(0, 3)
-                if n == 2:
-                    load_w(6)
-                    load_w(7)
-                    load_x(0)
-                    load_g(1, 0)
-                    load_x(1)
-                    load_g(1, 1)
-                    load_g(1, 2)
-                    load_g(1, 3)
-            feat_transpose(0, c)
-            feat_evac(0, c)
-            if c > 0:
-                feat_quant(0, c - 1)
-        x_copy(0, "S")
-        for c in range(FC):
-            w_quant(c)
-            if c == 1:
-                feat_quant(0, FC - 1)
-        tok_copy(0, 0, "V")
-        rope_sin(1, 0)
-        x_quant(0)
-        rope_cos(1, 0)
-        tok_quant(0, 0)
-        for j in range(4):
-            out0(0, j, "SS")
-            if j == 1:
-                x_copy(1, "S")
-        for c in range(FC):
-            if c < FC - 1:
-                rope_sin(1, c + 1)
-            rope_add(1, c)
-            if c == 0:
-                x_quant(1)
-            if c < FC - 1:
-                rope_cos(1, c + 1)
-            feat_transpose(1, c)
-            feat_evac(1, c)
-            if c == 0:
-                tok_copy(0, 1, "S")
-            tok_copy(1, c, "V")
-            if c < FC - 1:
-                tok_quant(0, c + 1)
-                feat_quant(1, c)
-            tok_quant(1, c)
-            if c == FC - 1:
-                feat_quant(1, c)
-            if c == FC - 1:
-                set_ring("acc", [2, 3, 0, 1])
-            for n2 in range(4):
-                out1(c, n2, "SS" if c < FC - 1 else "SV")
-                if n2 == 1 and c < FC - 2:
-                    tok_copy(0, c + 2, "S")
-            if c == 1:
-                set_ring("acc", [4, 5, 6, 7])
-                for j, n in ((0, 0), (0, 1), (1, 0), (1, 1)):
-                    out0_passes(1, j, n, (0, 1))
-                set_ring("acc", [2, 3])
-            if c == 2:
-                for j, n in ((0, 0), (0, 1), (1, 0), (1, 1)):
-                    out0_passes(1, j, n, (2,))
-        set_ring("acc", [2, 3, 0, 1, 4, 5, 6, 7])
-        for j in range(4):
-            if j < 2:
-                for n in range(2):
-                    out0_passes(1, j, n, (3,))
-                out0_store(1, j, "SV")
-            else:
-                out0(1, j, "SV")
+        with tc.manual_schedule():
+            for step in ORDER.split():
+                name, args, eng, b = step.split(":")
+                a = [int(d) for d in args]
+                b = int(b)
+                if name == "Lg":
+                    load_g(*a)
+                elif name == "Lw":
+                    load_w(*a)
+                elif name == "Lx":
+                    load_x(*a)
+                elif name == "TAB":
+                    tables()
+                elif name == "QS":
+                    rope_sin(*a)
+                elif name == "QC":
+                    rope_cos(*a)
+                elif name == "A":
+                    rope_add(*a)
+                elif name == "FT":
+                    feat_transpose(*a, b)
+                elif name == "FE":
+                    feat_evac(*a, eng)
+                elif name == "FQ":
+                    feat_quant(*a)
+                elif name == "TN":
+                    tok_copy(*a, 0, eng)
+                elif name == "TR":
+                    tok_copy(*a, 1, eng)
+                elif name == "TQ":
+                    tok_quant(*a)
+                elif name == "WT":
+                    w_transpose(*a, b)
+                elif name == "WE":
+                    w_evac(*a, eng)
+                elif name == "WQ":
+                    w_quant(*a)
+                elif name == "XC" and XM:
+                    x_evac(*a, eng)
+                elif name == "XM":
+                    x_move(*a, b)
+                elif name == "XC":
+                    x_copy(*a, eng)
+                elif name == "XQ":
+                    x_quant(*a)
+                elif name == "O":
+                    out0_pass(*a, b)
+                elif name == "OE":
+                    out0_evac(*a, eng)
+                elif name == "ZO":
+                    out0_store(*a)
+                elif name == "P":
+                    out1_group(*a, b)
+                elif name == "PE":
+                    out1_evac(*a, eng)
+                elif name == "ZP":
+                    out1_store(*a)

@@ -14,394 +14,323 @@ E5M2 = mybir.dt.float8_e5m2_x4
 ADD = mybir.AluOpType.add
 SUB = mybir.AluOpType.subtract
 MULT = mybir.AluOpType.mult
-IS_GE = mybir.AluOpType.is_ge
 SIN = mybir.ActivationFunctionType.Sin
 
 P = 128
 T = 1024
 D = 1024
 J = 2048
-S = 256
+SEQ = 256
 HEAD = 256
 ROPE = 128
+PAIRS = ROPE // 2
 K_PASS = 512
-TG = T // K_PASS
-FC = J // K_PASS
-HPC = K_PASS // HEAD
+GROUPS = T // K_PASS
+ROWS = 4
+CHUNKS = J // K_PASS
+HALF = J // 2
+HALF_HEADS = HALF // HEAD
 ROPE_BASE = 10000.0
-TGB = 4
-XM = False
-B4 = False
-FGB = 4
-RESB = 5
-WB = 4
-ORDER = (
-    "TAB::V:9 Lg:00:D:9 Lx:00:D:9 Lw:6:D:9 TN:00:V:9 Lg:01:D:9 XC:00:S:9 QC:00:V:9 Lw:4:D:9 WT:61:D:0 "
-    "QS:00:V:9 WT:60:D:1 Lw:3:D:9 QS:01:V:9 TN:01:S:9 Lg:02:D:9 WT:40:D:2 A:00:V:9 WE:61:S:9 WT:41:D:3 "
-    "Lw:0:D:9 WE:40:S:9 QC:01:V:9 FT:000:D:4 WE:41:S:9 Lw:2:D:9 WT:31:D:5 FE:000:S:9 QS:02:V:9 FT:001:D:6 "
-    "WE:60:S:9 Lw:1:D:9 WT:30:D:7 FE:001:S:9 QC:02:V:9 WT:01:D:0 Lg:03:D:9 WE:30:S:9 WT:00:D:2 WE:31:S:9 "
-    "A:01:V:9 WT:21:D:3 Lw:5:D:9 TR:00:S:9 WT:20:D:4 A:02:V:9 WT:11:D:1 Lw:7:D:9 FT:011:D:6 WE:20:S:9 "
-    "QS:03:V:9 FT:020:D:7 WE:01:S:9 Lg:13:D:9 WT:10:D:5 FE:011:S:9 QC:03:V:9 FT:010:D:4 WE:21:S:9 Lg:10:D:9 "
-    "WT:50:D:0 TR:01:S:9 FQ:00:V:9 WT:70:D:6 Lx:10:D:9 XQ:00:V:9 WT:51:D:3 WE:10:S:9 A:03:V:9 WE:50:S:9 "
-    "Lx:11:D:9 FT:021:D:5 WE:70:S:9 WT:71:D:0 QC:10:V:9 WE:00:S:9 Lg:12:D:9 FT:031:D:6 FE:021:S:9 FT:030:D:2 "
-    "WQ:0:V:9 FE:010:S:9 Lx:01:D:9 WE:71:S:9 FQ:01:V:9 O:0010:D:5 WE:11:S:9 Lg:11:D:9 O:0310:D:4 WQ:1:V:9 "
-    "O:0110:D:0 WE:51:S:9 O:0000:D:1 FE:020:S:9 O:0210:D:3 WQ:2:V:9 FE:031:S:9 O:0300:D:7 FE:030:S:9 "
-    "O:0100:D:6 WQ:3:V:9 O:0301:D:9 XC:10:S:9 O:0111:D:9 O:0200:D:2 O:0311:D:9 O:0201:D:9 FQ:02:V:9 O:0011:D:9 "
-    "O:0211:D:9 FQ:03:V:9 O:0302:D:9 O:0001:D:9 QS:10:V:9 O:0303:D:9 XC:01:S:9 O:0312:D:9 O:0202:D:9 "
-    "O:0101:D:9 XQ:10:V:9 O:0203:D:9 O:0212:D:9 QS:11:V:9 O:0102:D:9 O:0213:D:9 O:0103:D:9 O:0002:D:9 "
-    "QC:11:V:9 XC:11:S:9 O:0313:D:9 O:0012:D:9 O:0112:D:9 O:0113:D:9 TN:10:V:9 O:0013:D:9 A:10:V:9 OE:011:S:9 "
-    "A:11:V:9 OE:020:S:9 FT:101:D:0 OE:021:S:9 TR:10:V:9 FT:100:D:2 OE:001:S:9 ZO:02:D:9 FT:111:D:3 TQ:00:V:9 "
-    "OE:010:S:9 FT:110:D:5 TQ:10:V:9 FE:111:S:9 ZO:01:D:9 O:0003:D:9 XQ:01:V:9 FE:101:S:9 P:01:D:6 XQ:11:V:9 "
-    "OE:031:S:9 P:03:D:3 OE:030:V:9 FE:100:S:9 P:02:D:0 TN:11:V:9 TR:11:S:9 P:05:D:4 ZO:03:D:9 P:00:D:7 "
-    "OE:000:V:9 P:07:D:2 TQ:01:V:9 PE:00:S:9 ZO:00:D:9 P:06:D:1 TQ:11:V:9 FE:110:S:9 P:04:D:7 FQ:10:V:9 "
-    "PE:07:S:9 P:10:D:5 FQ:11:V:9 PE:06:S:9 P:11:D:2 QS:12:V:9 PE:01:S:9 ZP:03:D:9 P:13:D:1 PE:10:S:9 "
-    "O:1300:D:6 QC:13:V:9 PE:11:S:9 O:1301:D:9 ZP:00:D:9 P:15:D:5 PE:02:S:9 P:12:D:2 QC:12:V:9 PE:03:S:9 "
-    "ZP:10:D:9 O:1210:D:0 PE:04:S:9 O:1211:D:9 P:17:D:3 QS:13:V:9 PE:15:S:9 ZP:01:D:9 O:1200:D:7 PE:05:S:9 "
-    "O:1201:D:9 P:14:D:5 A:12:V:9 PE:13:S:9 ZP:02:D:9 O:1000:D:4 PE:14:S:9 O:1001:D:9 P:16:D:1 A:13:V:9 "
-    "PE:12:S:9 ZP:12:D:9 FT:121:D:5 PE:17:S:9 TN:12:V:9 FT:120:D:2 FE:121:S:9 ZP:11:D:9 FT:130:D:3 TN:02:V:9 "
-    "FE:120:S:9 FT:131:D:5 FE:130:S:9 FQ:12:V:9 O:1310:D:2 FE:131:S:9 O:1311:D:9 TR:02:V:9 O:1010:D:3 "
-    "TR:12:S:9 O:1312:D:9 FQ:13:V:9 O:1011:D:9 O:1002:D:9 TQ:02:V:9 O:1302:D:9 O:1202:D:9 TR:03:S:9 PE:16:V:9 "
-    "O:1203:D:9 O:1212:D:9 TQ:12:V:9 O:1303:D:9 ZP:13:D:9 O:1313:D:9 OE:130:S:9 O:1012:D:9 OE:131:V:9 "
-    "O:1213:D:9 TN:13:S:9 O:1003:D:9 OE:120:V:9 P:23:D:5 ZO:13:D:9 OE:121:V:9 P:22:D:1 PE:23:S:9 OE:100:V:9 "
-    "O:1013:D:9 ZO:12:D:9 P:27:D:6 TN:03:S:9 PE:22:V:9 P:26:D:2 TR:13:V:9 ZP:21:D:9 P:24:D:7 OE:101:V:9 "
-    "PE:27:S:9 P:21:D:0 TQ:13:V:9 PE:26:S:9 ZO:10:D:9 P:25:D:5 PE:24:S:9 TQ:03:V:9 P:20:D:4 PE:21:S:9 "
-    "ZP:23:D:9 P:33:D:1 PE:20:V:9 P:31:D:3 PE:25:V:9 ZP:20:D:9 P:32:D:6 P:34:D:2 PE:32:S:9 ZP:22:D:9 P:37:D:7 "
-    "PE:33:S:9 P:30:D:0 PE:31:S:9 ZP:31:D:9 O:1100:D:4 PE:30:V:9 PE:37:S:9 P:35:D:5 PE:34:S:9 O:1110:D:6 "
-    "ZP:30:D:9 O:1101:D:9 PE:35:S:9 P:36:D:1 O:1102:D:9 ZP:32:D:9 PE:36:S:9 O:1103:D:9 O:1111:D:9 OE:110:S:9 "
-    "O:1112:D:9 O:1113:D:9 ZP:33:D:9 OE:111:V:9 ZO:11:D:9 "
-)
+TWO_PI = 2.0 * math.pi
 FLOPS = 2 * 2 * T * D * J
+
+BUFFERS = {"bank": 8, "w": 4, "hs": 4, "hc": 4, "fg": 4, "tg": 4, "xg": 2, "res": 5}
+
+ORDER = (
+    "tab.. lg.01. lw.5. lg.03. rc.010. lw.4. rs.010. rc.011. wt.50. lw.3. ra.010. wt.51. we.50.S rs.011. ft.010.",
+    "lg.00. rc.030. fe.010.S rc.031. wt.41. lw.1. we.51.S rs.030. wt.40. we.41.S ra.011. wt.30. lw.2. we.40.S",
+    "ra.030. wt.31. we.30.S rs.031. ft.011. lg.11. we.31.S rc.001. ft.030. fe.011.S ra.031. wt.10. fe.030.S lw.7.",
+    "rc.000. wt.11. we.10.S rs.001. wt.20. we.11.S lw.6. rs.000. ft.031. ra.001. we.20.S wt.21. ra.000. fe.031.S",
+    "lw.0. ft.001. rs.111. we.21.S wt.70. rc.111. fe.001.S lg.10. wt.71. rc.110. we.70.S wt.61. rs.110. we.71.S",
+    "lx.0. wt.60. ra.111. we.61.S ft.000. fq.010. we.60.S ra.110. ft.111. fe.000.S fq.031. wt.00. fq.001. lx.1.",
+    "fe.111.S ft.110. fq.030. rs.100. we.00.S wt.01. rc.100. fe.110.S fq.011. we.01.S fq.000. lg.13. ra.100.",
+    "xc.01.S wq.0. ft.100. lg.12. wq.1. om.0100. fe.100.S lg.02. om.0000. om.0010. xc.10.S wq.2. om.0300. om.0310.",
+    "om.0011. om.0101. xq.01. om.0001. om.0110. wq.3. om.0311. xc.11.S om.0111. om.0301. om.0002. rs.131. om.0102.",
+    "om.0302. rs.130. om.0103. om.0112. rc.130. om.0113. oe.010.S om.0303. rc.131. om.0003. oe.011.S om.0312.",
+    "ra.130. om.0313. oe.000.S om.0012. os.01. ra.131. om.0013. oe.030.S ft.130. rs.020. oe.001.S ft.131. rc.020.",
+    "oe.031.S os.00. fq.110. fe.130.S fq.100. om.1110. ra.020. fe.131.S om.1100. os.03. rs.120. om.1000. tc.00.S",
+    "om.1010. rc.120. om.1101. om.1111. fq.130. om.1001. fq.111. om.1310. ra.120. om.1311. om.1102. fq.131.",
+    "om.1103. tc.11.S tc.01.V om.1300. om.1312. om.1313. om.1112. xq.11. om.1301. om.1302. tq.01. om.1303.",
+    "oe.110.S om.1113. tc.10.V ft.020. oe.130.S ft.120. oe.131.S tq.11. om.1011. xc.00.S fe.020.V os.13. pm.15.",
+    "oe.111.V pm.16. tq.10. os.11. pm.17. tq.00. pe.16.S pm.14. xq.10. pe.17.S pm.05. rc.021. pe.14.S pm.06.",
+    "ps.13. xq.00. pe.15.S pm.04. rs.121. pe.05.S pm.07. ps.12. rc.121. pe.04.S pm.12. rs.101. pe.06.S pm.01.",
+    "rs.021. fe.120.S ps.02. pm.13. rc.101. pe.07.S pm.02. ra.021. pe.01.S pm.00. ps.03. ra.121. pe.12.S ft.021.",
+    "ra.101. pe.13.S ft.121. fq.020. tc.02.S pe.00.V ps.11. ft.101. pe.02.V pm.03. fe.021.V pm.10. ps.00. fe.101.V",
+    "om.0210. pe.03.S om.0200. fq.021. om.0211. fq.101. pe.10.S pm.11. tc.12.V ps.01. fe.121.S om.1012. om.1013.",
+    "pe.11.S om.1002. tq.02. om.1003. oe.101.S om.0201. ps.10. tq.12. om.0212. oe.100.S om.0213. tc.13.V om.0202.",
+    "oe.021.S om.0203. os.10. pm.20. oe.020.S tc.03.V pm.21. pe.20.S os.02. pm.22. pe.21.S pm.23. tq.13. pe.22.S",
+    "pm.26. ps.20. tq.03. pe.23.S pm.27. fq.121. pe.26.S fq.120. pm.32. ps.21. pe.27.S pm.33. pe.32.S pm.34.",
+    "ps.23. pe.33.S pm.35. pe.34.S om.1200. pe.35.S pm.37. ps.31. pm.36. pe.37.S pm.25. ps.32. pe.36.V om.1201.",
+    "pe.25.S pm.24. pm.30. ps.33. pe.24.S om.1210. pe.30.S pm.31. ps.22. om.1211. pe.31.S om.1212. om.1213.",
+    "om.1202. oe.121.V om.1203. ph.30. ph.31. oe.120.S os.12.",
+)
 
 
 def tile_multiheadlatentattention_pb_v_kernel(tc, x, wq, grad_out, out_0, out_1):
     nc = tc.nc
-    x_v = x.rearrange("b s d -> (b s) d").rearrange("(g p j) d -> g p j d", g=TG, j=4)
-    g_v = grad_out.rearrange("b s h q -> (b s) (h q)").rearrange("(g p j) f -> g p j f", g=TG, j=4)
-    w_v = wq.rearrange("(n p) f -> n p f", p=P)
-    o0_v = out_0.rearrange("b s d -> (b s) d").rearrange("(g p j) d -> g p j d", g=TG, j=4)
-    o1_v = out_1.rearrange("(n p) f -> p n f", p=P)
+    x_rows = x.rearrange("b s d -> (b s) d").rearrange("(g p j) d -> g p j d", g=GROUPS, j=ROWS)
+    g_rows = grad_out.rearrange("b s h q -> (b s) (h q)").rearrange("(g p j) f -> g p j f", g=GROUPS, j=ROWS)
+    w_rows = wq.rearrange("(n p) f -> n p f", p=P)
+    out_0_rows = out_0.rearrange("b s d -> (b s) d").rearrange("(g p j) d -> g p j d", g=GROUPS, j=ROWS)
+    out_1_rows = out_1.rearrange("(n p) f -> p n f", p=P)
 
     with ExitStack() as ctx:
         keep = ctx.enter_context(tc.tile_pool(name="keep", bufs=1))
-        work = ctx.enter_context(tc.tile_pool(name="work", bufs=2))
+        work = ctx.enter_context(tc.tile_pool(name="work", bufs=1))
         psum = ctx.enter_context(tc.psum_pool(name="psum", bufs=1))
+        copy = {"V": nc.vector.tensor_copy, "S": nc.scalar.copy}
+        live = {}
 
-        g_sb = {}
-        x_sb = {}
-        w_sb = {}
-        tok_codes = {}
-        tok_scales = {}
-        feat_codes = {}
-        feat_scales = {}
-        x_codes = {}
-        x_scales = {}
-        w_codes = {}
-        w_scales = {}
-        mul_c = {}
-        mul_s = {}
-        grouped = {}
-        banks = {}
-        w_grp = {}
-        results = {}
+        idle = {kind: list(range(count)) for kind, count in BUFFERS.items()}
+        taken = {}
 
-        def tr_bank(b):
-            return psum.tile([P, 2, 2, P], F32, name="bank%d" % b, tag="bank%d" % b)
+        def take(kind, key, shape, dtype):
+            if (kind, key) not in live:
+                taken[kind, key] = idle[kind].pop(0)
+                tag = "%s%d" % (kind, taken[kind, key])
+                if kind == "bank":
+                    live[kind, key] = psum.tile(shape, dtype, name=tag, tag=tag)
+                else:
+                    live[kind, key] = work.tile(shape, dtype, name=tag, tag=tag, align_bytes=64)
+            return live[kind, key]
 
-        def acc_bank(b):
-            return psum.tile([P, K_PASS], F32, name="bank%d" % b, tag="bank%d" % b)
+        def give_back(kind, key):
+            idle[kind].append(taken[kind, key])
 
-        def copy(eng, dst, src):
-            if eng == "V":
-                nc.vector.tensor_copy(out=dst, in_=src)
-            else:
-                nc.scalar.copy(out=dst, in_=src)
+        def quantize(key, tag, width, fmt, src, cols):
+            if ("codes", key) not in live:
+                live["codes", key] = keep.tile([P, width], U32, name="codes_" + tag, tag="codes_" + tag, align_bytes=64)
+                live["scales", key] = keep.tile([P, width], U8, name="scales_" + tag, tag="scales_" + tag, align_bytes=64)
+            nc.vector.quantize_mx(out=live["codes", key][:, cols].bitcast(fmt), scales=live["scales", key][:, cols], in_=src)
 
-        def interleave(eng, dst, src):
-            if B4:
-                for h in range(HPC):
-                    copy(eng, dst[:, h].rearrange("p (k i) j -> p k j i", i=4), src[:, h].rearrange("p (k i) j -> p k j i", i=4))
-            else:
-                copy(eng, dst, src)
+        def multiply(out, left, left_cols, left_fmt, right, right_cols, right_fmt, first, last):
+            nc.tensor.matmul_mx(
+                out=out,
+                lhsT=live["codes", left][:, left_cols].bitcast(left_fmt),
+                lhsT_scale=live["scales", left][:, left_cols],
+                rhs=live["codes", right][:, right_cols].bitcast(right_fmt),
+                rhs_scale=live["scales", right][:, right_cols],
+                start=first,
+                stop=last,
+            )
 
-        def load_g(g, c):
-            t = keep.tile([P, 4, K_PASS], BF16, name="g%d%d" % (g, c), align_bytes=64)
-            nc.sync.dma_start(out=t[:], in_=g_v[g][:, :, c * K_PASS : (c + 1) * K_PASS])
-            g_sb[g, c] = t
+        def block(i, width):
+            return slice(i * width, (i + 1) * width)
 
-        def load_x(g, h):
-            t = keep.tile([P, 4, K_PASS], BF16, name="x%d%d" % (g, h), tag="x", bufs=3, align_bytes=64)
-            nc.sync.dma_start(out=t[:], in_=x_v[g][:, :, h * K_PASS : (h + 1) * K_PASS])
-            x_sb[g, h] = t
-
-        def load_w(n):
-            t = work.tile([P, J], BF16, name="w%d" % n, tag="w", bufs=WB, align_bytes=64)
-            nc.sync.dma_start(out=t[:], in_=w_v[n])
-            w_sb[n] = t
-
-        HALF = ROPE // 2
-        pos = keep.tile([P, 4], F32, name="pos")
-        freq = keep.tile([P, HALF], F32, name="freq")
-        turns = keep.tile([P, 2, 4 * HALF], F32, name="turns")
-        whole = keep.tile([P, 2, 4 * HALF], I32, name="whole")
-        cos_t = keep.tile([P, 4, ROPE], F32, name="cos_t")
-        sin_t = keep.tile([P, 4, ROPE], F32, name="sin_t")
+        pos = keep.tile([P, ROWS], F32, name="pos")
+        freq = keep.tile([P, PAIRS], F32, name="freq")
+        cos_t = keep.tile([P, ROWS, ROPE], F32, name="cos_t")
+        sin_t = keep.tile([P, ROWS, ROPE], F32, name="sin_t")
         ident = keep.tile([P, P], F32, name="ident")
-        ident_b = keep.tile([P, P], BF16, name="ident_b")
         warm = keep.tile([P, 1], F32, name="warm")
 
-        def tables():
+        def make_tables():
             nc.vector.memset(freq[:, 0:1], 1.0)
             nc.vector.memset(warm[:], 0.0)
             nc.scalar.activation(warm[:], warm[:], SIN)
             for q in range(2):
-                nc.gpsimd.iota(pos[q * 64 : (q + 1) * 64, :], pattern=[[1, 4]], base=0, channel_multiplier=4, allow_small_or_imprecise_dtypes=True)
+                nc.gpsimd.iota(
+                    pos[block(q, P // 2), :],
+                    pattern=[[1, ROWS]],
+                    base=0,
+                    channel_multiplier=ROWS,
+                    allow_small_or_imprecise_dtypes=True,
+                )
             make_identity(nc, ident[:])
-            if XM:
-                make_identity(nc, ident_b[:])
-            n = 1
-            while n < HALF:
-                nc.vector.tensor_scalar(out=freq[:, n : 2 * n], in0=freq[:, 0:n], scalar1=ROPE_BASE ** (-2.0 * n / ROPE), scalar2=None, op0=MULT)
-                n *= 2
-            nc.vector.scalar_tensor_tensor(
-                out=turns[:, 0].rearrange("p (j i) -> p j i", j=4),
-                in0=pos[:].unsqueeze(2).to_broadcast([P, 4, HALF]),
-                scalar=1.0 / (2.0 * math.pi),
-                in1=freq[:].unsqueeze(1).to_broadcast([P, 4, HALF]),
-                op0=MULT,
-                op1=MULT,
-            )
-            nc.vector.tensor_copy(out=whole[:, 0], in_=turns[:, 0])
+            for n in (1, 4, 16):
+                for k in range(n, 4 * n, n):
+                    nc.vector.tensor_scalar(
+                        out=freq[:, k : k + n], in0=freq[:, 0:n], scalar1=ROPE_BASE ** (-2.0 * k / ROPE), scalar2=None, op0=MULT
+                    )
+            turns = work.tile([P, 2, ROWS * PAIRS], F32, name="hs3", tag="hs3", align_bytes=64)
+            whole = work.tile([P, 2, ROWS * PAIRS], I32, name="hc3", tag="hc3", align_bytes=64)
+            for dst in (turns, whole):
+                nc.vector.scalar_tensor_tensor(
+                    out=dst[:, 0].rearrange("p (j i) -> p j i", j=ROWS),
+                    in0=pos[:].unsqueeze(2).to_broadcast([P, ROWS, PAIRS]),
+                    scalar=1.0 / TWO_PI,
+                    in1=freq[:].unsqueeze(1).to_broadcast([P, ROWS, PAIRS]),
+                    op0=MULT,
+                    op1=MULT,
+                )
             nc.vector.tensor_scalar(out=turns[:, 1], in0=turns[:, 0], scalar1=0.25, scalar2=None, op0=ADD)
             nc.vector.tensor_tensor(out=turns[:, 0], in0=turns[:, 0], in1=whole[:, 0], op=SUB)
             nc.vector.tensor_copy(out=whole[:, 1], in_=turns[:, 1])
-            two_pi = 2.0 * math.pi
             cos_v = cos_t[:].rearrange("p j (i e) -> p (j i) e", e=2)
             sin_v = sin_t[:].rearrange("p j (i e) -> p (j i) e", e=2)
-            nc.scalar.activation(sin_v[:, :, 1], turns[:, 0], SIN, scale=two_pi)
-            nc.scalar.activation(sin_v[:, :, 0], turns[:, 0], SIN, scale=-two_pi)
+            nc.scalar.activation(sin_v[:, :, 1], turns[:, 0], SIN, scale=TWO_PI)
+            nc.scalar.activation(sin_v[:, :, 0], turns[:, 0], SIN, scale=-TWO_PI)
             nc.vector.tensor_tensor(out=turns[:, 1], in0=turns[:, 1], in1=whole[:, 1], op=SUB)
-            nc.scalar.activation(cos_v, turns[:, 1].unsqueeze(2).to_broadcast([P, 4 * HALF, 2]), SIN, scale=two_pi)
+            nc.scalar.activation(cos_v, turns[:, 1].unsqueeze(2).to_broadcast([P, ROWS * PAIRS, 2]), SIN, scale=TWO_PI)
 
-        def rope_view(t):
-            return t[:].rearrange("p j (h q) -> p j h q", h=HPC)[:, :, :, HEAD - ROPE :]
+        dq = [keep.tile([P, ROWS, J], BF16, name="dq%d" % g, align_bytes=64) for g in range(GROUPS)]
+        x_sb = [keep.tile([P, ROWS, D], BF16, name="x%d" % g, align_bytes=64) for g in range(GROUPS)]
+        w_grouped = [keep.tile([P, 2, D, 4], BF16, name="w_grouped%d" % h, align_bytes=64) for h in range(2)]
 
-        def table_view(t):
-            return t[:].unsqueeze(2).to_broadcast([P, 4, HPC, ROPE])
+        def load_g(g, j):
+            nc.sync.dma_start(out=dq[g][:, j, :], in_=g_rows[g][:, j, :])
 
-        def rope_sin(g, c):
-            t = work.tile([P, 4, HPC, ROPE], F32, name="ms%d%d" % (g, c), tag="ms", bufs=2)
-            nc.vector.tensor_tensor(out=t[:], in0=rope_view(g_sb[g, c]), in1=table_view(sin_t), op=MULT)
-            mul_s[g, c] = t
+        def load_x(g):
+            nc.sync.dma_start(out=x_sb[g][:], in_=x_rows[g])
 
-        def rope_cos(g, c):
-            t = work.tile([P, 4, HPC, ROPE], F32, name="mc%d%d" % (g, c), tag="mc", bufs=2)
-            nc.vector.tensor_tensor(out=t[:], in0=rope_view(g_sb[g, c]), in1=table_view(cos_t), op=MULT)
-            mul_c[g, c] = t
+        def load_w(n):
+            nc.sync.dma_start(out=take("w", n, [P, J], BF16)[:], in_=w_rows[n])
 
-        def rope_add(g, c):
-            rows = g_sb[g, c][:].rearrange("p j (h q) -> p (j h) q", h=HPC)[:, :, HEAD - ROPE :]
+        def rope_values(g, j, h):
+            return dq[g][:, j, block(h, HALF)].rearrange("p (n q) -> p n q", n=HALF_HEADS)[:, :, HEAD - ROPE :]
+
+        def rope_product(kind, table, g, j, h):
             nc.vector.tensor_tensor(
-                out=rows.rearrange("p r (i e) -> p r i e", e=2),
-                in0=mul_c[g, c][:].rearrange("p j h (i e) -> p (j h) i e", e=2),
-                in1=mul_s[g, c][:].rearrange("p j h (i e) -> p (j h) i e", e=2)[:, :, :, ::-1],
+                out=take(kind, (g, j, h), [P, HALF_HEADS, ROPE], F32)[:],
+                in0=rope_values(g, j, h),
+                in1=table[:, j].unsqueeze(1).to_broadcast([P, HALF_HEADS, ROPE]),
+                op=MULT,
+            )
+
+        def rope_sin(g, j, h):
+            rope_product("hs", sin_t, g, j, h)
+
+        def rope_cos(g, j, h):
+            rope_product("hc", cos_t, g, j, h)
+
+        def rope_add(g, j, h):
+            by_pair = [live[kind, (g, j, h)][:].rearrange("p n (i e) -> p n i e", e=2) for kind in ("hc", "hs")]
+            nc.vector.tensor_tensor(
+                out=rope_values(g, j, h).rearrange("p n (i e) -> p n i e", e=2),
+                in0=by_pair[0],
+                in1=by_pair[1][:, :, :, ::-1],
                 op=ADD,
             )
+            give_back("hc", (g, j, h))
+            give_back("hs", (g, j, h))
 
-        def tok_copy(g, c, half, eng):
-            if ("t", g, c) not in grouped:
-                grouped["t", g, c] = work.tile([P, K_PASS, 4], BF16, name="tg%d%d" % (g, c), tag="tg", bufs=TGB, align_bytes=64)
-            src = g_sb[g, c][:].rearrange("p j (h q) -> p h q j", h=HPC)[:, :, half * ROPE : (half + 1) * ROPE, :]
-            dst = grouped["t", g, c][:].rearrange("p (h q) j -> p h q j", h=HPC)[:, :, half * ROPE : (half + 1) * ROPE, :]
-            interleave(eng, dst, src)
-
-        def flat(t):
-            return t[:].rearrange("p a b -> p (a b)")
-
-        def tok_quant(g, c):
-            q = keep.tile([P, K_PASS], U32, name="tq%d%d" % (g, c), tag="tq%d%d" % (g, c % 2 if g else c), align_bytes=64)
-            s = keep.tile([P, K_PASS], U8, name="ts%d%d" % (g, c), tag="ts%d%d" % (g, c % 2 if g else c), align_bytes=64)
-            nc.vector.quantize_mx(out=q[:].bitcast(E5M2), scales=s[:], in_=flat(grouped["t", g, c]))
-            tok_codes[g, c] = q
-            tok_scales[g, c] = s
-
-        def feat_transpose(g, c, half, b):
-            words = g_sb[g, c][:].rearrange("p j f -> p (j f)").bitcast(F32)
-            bank = tr_bank(b)
-            for jj in range(2):
-                base = (2 * half + jj) * (K_PASS // 2)
+        def transpose_chunks(bank, words, half):
+            for c in range(2):
+                first = (2 * half + c) * (K_PASS // 2)
                 for u in range(2):
-                    nc.tensor.transpose(bank[:, jj, u, :], words[:, base + u : base + K_PASS // 2 : 2], ident[:])
-            banks["f", g, c, half] = bank
+                    nc.tensor.transpose(bank[:, c, u, :], words[:, first + u : first + K_PASS // 2 : 2], ident[:])
 
-        def feat_evac(g, c, half, eng):
-            if ("f", g, c) not in grouped:
-                grouped["f", g, c] = work.tile([P, K_PASS, 4], BF16, name="fg%d%d" % (g, c), tag="fg", bufs=FGB, align_bytes=64)
-            words = flat(grouped["f", g, c]).bitcast(F32)
-            copy(
-                eng,
-                words[:, half * K_PASS : (half + 1) * K_PASS].rearrange("p (j r u) -> p j r u", j=2, u=2),
-                banks["f", g, c, half][:].rearrange("p j u r -> p j r u"),
+        def interleave_words(engine, dst, bank):
+            copy[engine](
+                out=dst.rearrange("p c (r u) -> p c r u", u=2),
+                in_=bank[:].rearrange("p c u r -> p c r u"),
             )
 
-        def feat_quant(g, c):
-            q = keep.tile([P, K_PASS], U32, name="fq%d%d" % (g, c), tag="fq%d" % (c if g == 0 or c > 1 else c + 4), align_bytes=64)
-            s = keep.tile([P, K_PASS], U8, name="fs%d%d" % (g, c), tag="fs%d" % (c if g == 0 or c > 1 else c + 4), align_bytes=64)
-            nc.vector.quantize_mx(out=q[:].bitcast(E5M2), scales=s[:], in_=flat(grouped["f", g, c]))
-            feat_codes[g, c] = q
-            feat_scales[g, c] = s
+        def feature_transpose(g, j, h):
+            bank = take("bank", ("f", g, j, h), [P, 2, 2, P], F32)
+            transpose_chunks(bank, dq[g][:, j, :].bitcast(F32), h)
 
-        def w_transpose(n, half, b):
-            words = w_sb[n][:].bitcast(F32)
-            bank = tr_bank(b)
-            for cc in range(2):
-                base = (2 * half + cc) * (K_PASS // 2)
-                for u in range(2):
-                    nc.tensor.transpose(bank[:, cc, u, :], words[:, base + u : base + K_PASS // 2 : 2], ident[:])
-            banks["w", n, half] = bank
+        def feature_evacuate(g, j, h, engine):
+            grouped = take("fg", (g, j), [P, CHUNKS, P, 4], BF16)
+            words = grouped[:].rearrange("p c r t -> p c (r t)").bitcast(F32)
+            interleave_words(engine, words[:, block(h, 2)], live["bank", ("f", g, j, h)])
+            give_back("bank", ("f", g, j, h))
 
-        def w_evac(n, half, eng):
-            if half not in w_grp:
-                w_grp[half] = keep.tile([P, 2, D, 4], BF16, name="wg%d" % half, align_bytes=64)
-            words = w_grp[half][:].rearrange("p c d t -> p c (d t)").bitcast(F32)
-            copy(
-                eng,
-                words[:, :, n * 2 * P : (n + 1) * 2 * P].rearrange("p c (r u) -> p c r u", u=2),
-                banks["w", n, half][:].rearrange("p c u r -> p c r u"),
+        def feature_quantize(g, j, h):
+            src = live["fg", (g, j)][:, block(h, 2)].rearrange("p c r t -> p (c r t)")
+            done = ("codes", ("f", g, j)) in live
+            quantize(("f", g, j), "f%d" % j, K_PASS, E5M2, src, block(h, 2 * P))
+            if done:
+                give_back("fg", (g, j))
+
+        def w_transpose(n, h):
+            bank = take("bank", ("w", n, h), [P, 2, 2, P], F32)
+            done = ("bank", ("w", n, 1 - h)) in live
+            transpose_chunks(bank, live["w", n][:].bitcast(F32), h)
+            if done:
+                give_back("w", n)
+
+        def w_evacuate(n, h, engine):
+            words = w_grouped[h][:].rearrange("p c d t -> p c (d t)").bitcast(F32)
+            interleave_words(engine, words[:, :, block(n, 2 * P)], live["bank", ("w", n, h)])
+            give_back("bank", ("w", n, h))
+
+        def w_quantize(c):
+            src = w_grouped[c // 2][:].rearrange("p c d t -> p c (d t)")[:, c % 2]
+            quantize(("w", c), "w%d" % c, D, E4M3, src, block(0, D))
+
+        def interleave_rows(engine, dst, src):
+            copy[engine](
+                out=dst.rearrange("p (k i) j -> p k j i", i=4),
+                in_=src.rearrange("p j (k i) -> p k j i", i=4),
             )
 
-        def w_quant(c):
-            q = keep.tile([P, D], U32, name="wq%d" % c, align_bytes=64)
-            s = keep.tile([P, D], U8, name="ws%d" % c, align_bytes=64)
-            src = w_grp[c // 2][:].rearrange("p c d t -> p c (d t)")[:, c % 2]
-            nc.vector.quantize_mx(out=q[:].bitcast(E4M3), scales=s[:], in_=src)
-            w_codes[c] = q
-            w_scales[c] = s
+        def token_copy(g, c, engine):
+            interleave_rows(engine, take("tg", (g, c), [P, K_PASS, 4], BF16)[:], dq[g][:, :, block(c, K_PASS)])
 
-        def x_copy(g, h, eng):
-            t = work.tile([P, K_PASS, 4], BF16, name="xg%d%d" % (g, h), tag="xg", bufs=2, align_bytes=64)
-            interleave(eng, t[:].rearrange("p (h d) j -> p h d j", h=HPC), x_sb[g, h][:].rearrange("p j (h d) -> p h d j", h=HPC))
-            grouped["x", g, h] = t
+        def token_quantize(g, c):
+            src = live["tg", (g, c)][:].rearrange("p k j -> p (k j)")
+            quantize(("t", g, c), "t%d%d" % (g, c), K_PASS, E5M2, src, block(0, K_PASS))
+            give_back("tg", (g, c))
 
-        def x_move(g, h, k, b):
-            bank = psum.tile([P, 2, K_PASS], BF16, name="bank%d" % b, tag="bank%d" % b)
-            for q in range(2):
-                cols = slice((2 * k + q) * P, (2 * k + q + 1) * P)
-                nc.tensor.matmul(bank[:, q, :], lhsT=ident_b[:], rhs=x_sb[g, h][:, :, cols].rearrange("p j d -> p d j"), start=True, stop=True)
-            banks["x", g, h, k] = bank
+        def x_copy(g, h, engine):
+            interleave_rows(engine, take("xg", (g, h), [P, K_PASS, 4], BF16)[:], x_sb[g][:, :, block(h, K_PASS)])
 
-        def x_evac(g, h, k, eng):
-            if ("x", g, h) not in grouped:
-                grouped["x", g, h] = work.tile([P, K_PASS, 4], BF16, name="xg%d%d" % (g, h), tag="xg", bufs=2, align_bytes=64)
-            copy(eng, flat(grouped["x", g, h])[:, k * 1024 : (k + 1) * 1024], banks["x", g, h, k][:].rearrange("p a b -> p (a b)"))
+        def x_quantize(g, h):
+            src = live["xg", (g, h)][:].rearrange("p k j -> p (k j)")
+            quantize(("x", g, h), "x%d%d" % (g, h), K_PASS, E4M3, src, block(0, K_PASS))
+            give_back("xg", (g, h))
 
-        def x_quant(g, h):
-            q = keep.tile([P, K_PASS], U32, name="xq%d%d" % (g, h), align_bytes=64)
-            s = keep.tile([P, K_PASS], U8, name="xs%d%d" % (g, h), align_bytes=64)
-            nc.vector.quantize_mx(out=q[:].bitcast(E4M3), scales=s[:], in_=flat(grouped["x", g, h]))
-            x_codes[g, h] = q
-            x_scales[g, h] = s
+        def out_0_pass(g, j, n, c):
+            acc = take("bank", ("o", g, j, n), [P, K_PASS], F32)
+            multiply(acc[:], ("f", g, j), block(c, P), E5M2, ("w", c), block(n, K_PASS), E4M3, c == 0, c == CHUNKS - 1)
 
-        def out0_pass(g, j, n, c, b):
-            rows = slice(j * P, (j + 1) * P)
-            cols = slice(n * K_PASS, (n + 1) * K_PASS)
-            if c == 0:
-                banks["o", g, j, n] = acc_bank(b)
-            nc.tensor.matmul_mx(
-                out=banks["o", g, j, n][:],
-                lhsT=feat_codes[g, c][:, rows].bitcast(E5M2),
-                lhsT_scale=feat_scales[g, c][:, rows],
-                rhs=w_codes[c][:, cols].bitcast(E4M3),
-                rhs_scale=w_scales[c][:, cols],
-                start=(c == 0),
-                stop=(c == FC - 1),
-            )
+        def out_0_evacuate(g, j, n, engine):
+            res = take("res", ("o", g, j), [P, 2, K_PASS], F32)
+            copy[engine](out=res[:, n], in_=live["bank", ("o", g, j, n)][:])
+            give_back("bank", ("o", g, j, n))
 
-        def result(key):
-            if key not in results:
-                results[key] = work.tile([P, 2, K_PASS], F32, name="res", tag="res", bufs=RESB)
-            return results[key]
+        def out_0_store(g, j):
+            nc.sync.dma_start(out=out_0_rows[g][:, j, :], in_=live["res", ("o", g, j)][:].rearrange("p n k -> p (n k)"))
+            give_back("res", ("o", g, j))
 
-        def out0_evac(g, j, n, eng):
-            copy(eng, result(("o", g, j))[:, n], banks["o", g, j, n][:])
+        def out_1_passes(c, d):
+            acc = take("bank", ("p", c, d), [P, K_PASS], F32)
+            for g in range(GROUPS):
+                left = ("x", g, d // 4)
+                multiply(acc[:], left, block(d % 4, P), E4M3, ("t", g, c), block(0, K_PASS), E5M2, g == 0, g == GROUPS - 1)
 
-        def out0_store(g, j):
-            nc.sync.dma_start(out=o0_v[g][:, j, :], in_=result(("o", g, j))[:].rearrange("p n d -> p (n d)"))
+        def out_1_evacuate(c, d, engine):
+            res = take("res", ("p", c, d // 2), [P, 2, K_PASS], F32)
+            copy[engine](out=res[:, d % 2], in_=live["bank", ("p", c, d)][:])
+            give_back("bank", ("p", c, d))
 
-        def out1_group(c, dt, b):
-            acc = acc_bank(b)
-            cols = slice(dt % 4 * P, (dt % 4 + 1) * P)
-            for g in range(TG):
-                nc.tensor.matmul_mx(
-                    out=acc[:],
-                    lhsT=x_codes[g, dt // 4][:, cols].bitcast(E4M3),
-                    lhsT_scale=x_scales[g, dt // 4][:, cols],
-                    rhs=tok_codes[g, c][:].bitcast(E5M2),
-                    rhs_scale=tok_scales[g, c][:],
-                    start=(g == 0),
-                    stop=(g == TG - 1),
-                )
-            banks["p", c, dt] = acc
+        def out_1_store(c, k):
+            nc.sync.dma_start(out=out_1_rows[:, block(k, 2), block(c, K_PASS)], in_=live["res", ("p", c, k)][:])
+            give_back("res", ("p", c, k))
 
-        def out1_evac(c, dt, eng):
-            copy(eng, result(("p", c, dt // 2))[:, dt % 2], banks["p", c, dt][:])
+        def out_1_store_half(c, d):
+            nc.sync.dma_start(out=out_1_rows[:, d, block(c, K_PASS)], in_=live["res", ("p", c, d // 2)][:, d % 2])
 
-        def out1_store(c, k):
-            nc.sync.dma_start(out=o1_v[:, 2 * k : 2 * k + 2, c * K_PASS : (c + 1) * K_PASS], in_=result(("p", c, k))[:])
-
+        steps = {
+            "tab": make_tables,
+            "lg": load_g,
+            "lw": load_w,
+            "lx": load_x,
+            "rs": rope_sin,
+            "rc": rope_cos,
+            "ra": rope_add,
+            "ft": feature_transpose,
+            "fe": feature_evacuate,
+            "fq": feature_quantize,
+            "tc": token_copy,
+            "tq": token_quantize,
+            "wt": w_transpose,
+            "we": w_evacuate,
+            "wq": w_quantize,
+            "xc": x_copy,
+            "xq": x_quantize,
+            "om": out_0_pass,
+            "oe": out_0_evacuate,
+            "os": out_0_store,
+            "pm": out_1_passes,
+            "pe": out_1_evacuate,
+            "ps": out_1_store,
+            "ph": out_1_store_half,
+        }
         with tc.manual_schedule():
-            for step in ORDER.split():
-                name, args, eng, b = step.split(":")
-                a = [int(d) for d in args]
-                b = int(b)
-                if name == "Lg":
-                    load_g(*a)
-                elif name == "Lw":
-                    load_w(*a)
-                elif name == "Lx":
-                    load_x(*a)
-                elif name == "TAB":
-                    tables()
-                elif name == "QS":
-                    rope_sin(*a)
-                elif name == "QC":
-                    rope_cos(*a)
-                elif name == "A":
-                    rope_add(*a)
-                elif name == "FT":
-                    feat_transpose(*a, b)
-                elif name == "FE":
-                    feat_evac(*a, eng)
-                elif name == "FQ":
-                    feat_quant(*a)
-                elif name == "TN":
-                    tok_copy(*a, 0, eng)
-                elif name == "TR":
-                    tok_copy(*a, 1, eng)
-                elif name == "TQ":
-                    tok_quant(*a)
-                elif name == "WT":
-                    w_transpose(*a, b)
-                elif name == "WE":
-                    w_evac(*a, eng)
-                elif name == "WQ":
-                    w_quant(*a)
-                elif name == "XC" and XM:
-                    x_evac(*a, eng)
-                elif name == "XM":
-                    x_move(*a, b)
-                elif name == "XC":
-                    x_copy(*a, eng)
-                elif name == "XQ":
-                    x_quant(*a)
-                elif name == "O":
-                    out0_pass(*a, b)
-                elif name == "OE":
-                    out0_evac(*a, eng)
-                elif name == "ZO":
-                    out0_store(*a)
-                elif name == "P":
-                    out1_group(*a, b)
-                elif name == "PE":
-                    out1_evac(*a, eng)
-                elif name == "ZP":
-                    out1_store(*a)
+            for line in ORDER:
+                for step in line.split():
+                    name, indices, engine = step.split(".")
+                    arguments = [int(i) for i in indices] + ([engine] if engine else [])
+                    steps[name](*arguments)

import math
from contextlib import ExitStack

import concourse.mybir as mybir
from concourse.masks import make_identity

F32 = mybir.dt.float32
BF16 = mybir.dt.bfloat16
I32 = mybir.dt.int32
U32 = mybir.dt.uint32
U8 = mybir.dt.uint8
E4M3 = mybir.dt.float8_e4m3fn_x4
E5M2 = mybir.dt.float8_e5m2_x4
ADD = mybir.AluOpType.add
SUB = mybir.AluOpType.subtract
MULT = mybir.AluOpType.mult
SIN = mybir.ActivationFunctionType.Sin

P = 128
T = 1024
D = 1024
J = 2048
SEQ = 256
HEAD = 256
ROPE = 128
PAIRS = ROPE // 2
K_PASS = 512
GROUPS = T // K_PASS
ROWS = 4
CHUNKS = J // K_PASS
HALF = J // 2
HALF_HEADS = HALF // HEAD
ROPE_BASE = 10000.0
TWO_PI = 2.0 * math.pi
FLOPS = 2 * 2 * T * D * J

BUFFERS = {"bank": 8, "w": 4, "hs": 4, "hc": 4, "fg": 4, "tg": 4, "xg": 2, "res": 5}

ORDER = (
    "tab.. lg.01. lw.5. lg.03. rc.010. lw.4. rs.010. rc.011. wt.50. lw.3. ra.010. wt.51. we.50.S rs.011. ft.010.",
    "lg.00. rc.030. fe.010.S rc.031. wt.41. lw.1. we.51.S rs.030. wt.40. we.41.S ra.011. wt.30. lw.2. we.40.S",
    "ra.030. wt.31. we.30.S rs.031. ft.011. lg.11. we.31.S rc.001. ft.030. fe.011.S ra.031. wt.10. fe.030.S lw.7.",
    "rc.000. wt.11. we.10.S rs.001. wt.20. we.11.S lw.6. rs.000. ft.031. ra.001. we.20.S wt.21. ra.000. fe.031.S",
    "lw.0. ft.001. rs.111. we.21.S wt.70. rc.111. fe.001.S lg.10. wt.71. rc.110. we.70.S wt.61. rs.110. we.71.S",
    "lx.0. wt.60. ra.111. we.61.S ft.000. fq.010. we.60.S ra.110. ft.111. fe.000.S fq.031. wt.00. fq.001. lx.1.",
    "fe.111.S ft.110. fq.030. rs.100. we.00.S wt.01. rc.100. fe.110.S fq.011. we.01.S fq.000. lg.13. ra.100.",
    "xc.01.S wq.0. ft.100. lg.12. wq.1. om.0100. fe.100.S lg.02. om.0000. om.0010. xc.10.S wq.2. om.0300. om.0310.",
    "om.0011. om.0101. xq.01. om.0001. om.0110. wq.3. om.0311. xc.11.S om.0111. om.0301. om.0002. rs.131. om.0102.",
    "om.0302. rs.130. om.0103. om.0112. rc.130. om.0113. oe.010.S om.0303. rc.131. om.0003. oe.011.S om.0312.",
    "ra.130. om.0313. oe.000.S om.0012. os.01. ra.131. om.0013. oe.030.S ft.130. rs.020. oe.001.S ft.131. rc.020.",
    "oe.031.S os.00. fq.110. fe.130.S fq.100. om.1110. ra.020. fe.131.S om.1100. os.03. rs.120. om.1000. tc.00.S",
    "om.1010. rc.120. om.1101. om.1111. fq.130. om.1001. fq.111. om.1310. ra.120. om.1311. om.1102. fq.131.",
    "om.1103. tc.11.S tc.01.V om.1300. om.1312. om.1313. om.1112. xq.11. om.1301. om.1302. tq.01. om.1303.",
    "oe.110.S om.1113. tc.10.V ft.020. oe.130.S ft.120. oe.131.S tq.11. om.1011. xc.00.S fe.020.V os.13. pm.15.",
    "oe.111.V pm.16. tq.10. os.11. pm.17. tq.00. pe.16.S pm.14. xq.10. pe.17.S pm.05. rc.021. pe.14.S pm.06.",
    "ps.13. xq.00. pe.15.S pm.04. rs.121. pe.05.S pm.07. ps.12. rc.121. pe.04.S pm.12. rs.101. pe.06.S pm.01.",
    "rs.021. fe.120.S ps.02. pm.13. rc.101. pe.07.S pm.02. ra.021. pe.01.S pm.00. ps.03. ra.121. pe.12.S ft.021.",
    "ra.101. pe.13.S ft.121. fq.020. tc.02.S pe.00.V ps.11. ft.101. pe.02.V pm.03. fe.021.V pm.10. ps.00. fe.101.V",
    "om.0210. pe.03.S om.0200. fq.021. om.0211. fq.101. pe.10.S pm.11. tc.12.V ps.01. fe.121.S om.1012. om.1013.",
    "pe.11.S om.1002. tq.02. om.1003. oe.101.S om.0201. ps.10. tq.12. om.0212. oe.100.S om.0213. tc.13.V om.0202.",
    "oe.021.S om.0203. os.10. pm.20. oe.020.S tc.03.V pm.21. pe.20.S os.02. pm.22. pe.21.S pm.23. tq.13. pe.22.S",
    "pm.26. ps.20. tq.03. pe.23.S pm.27. fq.121. pe.26.S fq.120. pm.32. ps.21. pe.27.S pm.33. pe.32.S pm.34.",
    "ps.23. pe.33.S pm.35. pe.34.S om.1200. pe.35.S pm.37. ps.31. pm.36. pe.37.S pm.25. ps.32. pe.36.V om.1201.",
    "pe.25.S pm.24. pm.30. ps.33. pe.24.S om.1210. pe.30.S pm.31. ps.22. om.1211. pe.31.S om.1212. om.1213.",
    "om.1202. oe.121.V om.1203. ph.30. ph.31. oe.120.S os.12.",
)


def tile_multiheadlatentattention_pb_v_kernel(tc, x, wq, grad_out, out_0, out_1):
    nc = tc.nc
    x_rows = x.rearrange("b s d -> (b s) d").rearrange("(g p j) d -> g p j d", g=GROUPS, j=ROWS)
    g_rows = grad_out.rearrange("b s h q -> (b s) (h q)").rearrange("(g p j) f -> g p j f", g=GROUPS, j=ROWS)
    w_rows = wq.rearrange("(n p) f -> n p f", p=P)
    out_0_rows = out_0.rearrange("b s d -> (b s) d").rearrange("(g p j) d -> g p j d", g=GROUPS, j=ROWS)
    out_1_rows = out_1.rearrange("(n p) f -> p n f", p=P)

    with ExitStack() as ctx:
        keep = ctx.enter_context(tc.tile_pool(name="keep", bufs=1))
        work = ctx.enter_context(tc.tile_pool(name="work", bufs=1))
        psum = ctx.enter_context(tc.psum_pool(name="psum", bufs=1))
        copy = {"V": nc.vector.tensor_copy, "S": nc.scalar.copy}
        live = {}

        idle = {kind: list(range(count)) for kind, count in BUFFERS.items()}
        taken = {}

        def take(kind, key, shape, dtype):
            if (kind, key) not in live:
                taken[kind, key] = idle[kind].pop(0)
                tag = "%s%d" % (kind, taken[kind, key])
                if kind == "bank":
                    live[kind, key] = psum.tile(shape, dtype, name=tag, tag=tag)
                else:
                    live[kind, key] = work.tile(shape, dtype, name=tag, tag=tag, align_bytes=64)
            return live[kind, key]

        def give_back(kind, key):
            idle[kind].append(taken[kind, key])

        def quantize(key, tag, width, fmt, src, cols):
            if ("codes", key) not in live:
                live["codes", key] = keep.tile([P, width], U32, name="codes_" + tag, tag="codes_" + tag, align_bytes=64)
                live["scales", key] = keep.tile([P, width], U8, name="scales_" + tag, tag="scales_" + tag, align_bytes=64)
            nc.vector.quantize_mx(out=live["codes", key][:, cols].bitcast(fmt), scales=live["scales", key][:, cols], in_=src)

        def multiply(out, left, left_cols, left_fmt, right, right_cols, right_fmt, first, last):
            nc.tensor.matmul_mx(
                out=out,
                lhsT=live["codes", left][:, left_cols].bitcast(left_fmt),
                lhsT_scale=live["scales", left][:, left_cols],
                rhs=live["codes", right][:, right_cols].bitcast(right_fmt),
                rhs_scale=live["scales", right][:, right_cols],
                start=first,
                stop=last,
            )

        def block(i, width):
            return slice(i * width, (i + 1) * width)

        pos = keep.tile([P, ROWS], F32, name="pos")
        freq = keep.tile([P, PAIRS], F32, name="freq")
        cos_t = keep.tile([P, ROWS, ROPE], F32, name="cos_t")
        sin_t = keep.tile([P, ROWS, ROPE], F32, name="sin_t")
        ident = keep.tile([P, P], F32, name="ident")
        warm = keep.tile([P, 1], F32, name="warm")

        def make_tables():
            nc.vector.memset(freq[:, 0:1], 1.0)
            nc.vector.memset(warm[:], 0.0)
            nc.scalar.activation(warm[:], warm[:], SIN)
            for q in range(2):
                nc.gpsimd.iota(
                    pos[block(q, P // 2), :],
                    pattern=[[1, ROWS]],
                    base=0,
                    channel_multiplier=ROWS,
                    allow_small_or_imprecise_dtypes=True,
                )
            make_identity(nc, ident[:])
            for n in (1, 4, 16):
                for k in range(n, 4 * n, n):
                    nc.vector.tensor_scalar(
                        out=freq[:, k : k + n], in0=freq[:, 0:n], scalar1=ROPE_BASE ** (-2.0 * k / ROPE), scalar2=None, op0=MULT
                    )
            turns = work.tile([P, 2, ROWS * PAIRS], F32, name="hs3", tag="hs3", align_bytes=64)
            whole = work.tile([P, 2, ROWS * PAIRS], I32, name="hc3", tag="hc3", align_bytes=64)
            for dst in (turns, whole):
                nc.vector.scalar_tensor_tensor(
                    out=dst[:, 0].rearrange("p (j i) -> p j i", j=ROWS),
                    in0=pos[:].unsqueeze(2).to_broadcast([P, ROWS, PAIRS]),
                    scalar=1.0 / TWO_PI,
                    in1=freq[:].unsqueeze(1).to_broadcast([P, ROWS, PAIRS]),
                    op0=MULT,
                    op1=MULT,
                )
            nc.vector.tensor_scalar(out=turns[:, 1], in0=turns[:, 0], scalar1=0.25, scalar2=None, op0=ADD)
            nc.vector.tensor_tensor(out=turns[:, 0], in0=turns[:, 0], in1=whole[:, 0], op=SUB)
            nc.vector.tensor_copy(out=whole[:, 1], in_=turns[:, 1])
            cos_v = cos_t[:].rearrange("p j (i e) -> p (j i) e", e=2)
            sin_v = sin_t[:].rearrange("p j (i e) -> p (j i) e", e=2)
            nc.scalar.activation(sin_v[:, :, 1], turns[:, 0], SIN, scale=TWO_PI)
            nc.scalar.activation(sin_v[:, :, 0], turns[:, 0], SIN, scale=-TWO_PI)
            nc.vector.tensor_tensor(out=turns[:, 1], in0=turns[:, 1], in1=whole[:, 1], op=SUB)
            nc.scalar.activation(cos_v, turns[:, 1].unsqueeze(2).to_broadcast([P, ROWS * PAIRS, 2]), SIN, scale=TWO_PI)

        dq = [keep.tile([P, ROWS, J], BF16, name="dq%d" % g, align_bytes=64) for g in range(GROUPS)]
        x_sb = [keep.tile([P, ROWS, D], BF16, name="x%d" % g, align_bytes=64) for g in range(GROUPS)]
        w_grouped = [keep.tile([P, 2, D, 4], BF16, name="w_grouped%d" % h, align_bytes=64) for h in range(2)]

        def load_g(g, j):
            nc.sync.dma_start(out=dq[g][:, j, :], in_=g_rows[g][:, j, :])

        def load_x(g):
            nc.sync.dma_start(out=x_sb[g][:], in_=x_rows[g])

        def load_w(n):
            nc.sync.dma_start(out=take("w", n, [P, J], BF16)[:], in_=w_rows[n])

        def rope_values(g, j, h):
            return dq[g][:, j, block(h, HALF)].rearrange("p (n q) -> p n q", n=HALF_HEADS)[:, :, HEAD - ROPE :]

        def rope_product(kind, table, g, j, h):
            nc.vector.tensor_tensor(
                out=take(kind, (g, j, h), [P, HALF_HEADS, ROPE], F32)[:],
                in0=rope_values(g, j, h),
                in1=table[:, j].unsqueeze(1).to_broadcast([P, HALF_HEADS, ROPE]),
                op=MULT,
            )

        def rope_sin(g, j, h):
            rope_product("hs", sin_t, g, j, h)

        def rope_cos(g, j, h):
            rope_product("hc", cos_t, g, j, h)

        def rope_add(g, j, h):
            by_pair = [live[kind, (g, j, h)][:].rearrange("p n (i e) -> p n i e", e=2) for kind in ("hc", "hs")]
            nc.vector.tensor_tensor(
                out=rope_values(g, j, h).rearrange("p n (i e) -> p n i e", e=2),
                in0=by_pair[0],
                in1=by_pair[1][:, :, :, ::-1],
                op=ADD,
            )
            give_back("hc", (g, j, h))
            give_back("hs", (g, j, h))

        def transpose_chunks(bank, words, half):
            for c in range(2):
                first = (2 * half + c) * (K_PASS // 2)
                for u in range(2):
                    nc.tensor.transpose(bank[:, c, u, :], words[:, first + u : first + K_PASS // 2 : 2], ident[:])

        def interleave_words(engine, dst, bank):
            copy[engine](
                out=dst.rearrange("p c (r u) -> p c r u", u=2),
                in_=bank[:].rearrange("p c u r -> p c r u"),
            )

        def feature_transpose(g, j, h):
            bank = take("bank", ("f", g, j, h), [P, 2, 2, P], F32)
            transpose_chunks(bank, dq[g][:, j, :].bitcast(F32), h)

        def feature_evacuate(g, j, h, engine):
            grouped = take("fg", (g, j), [P, CHUNKS, P, 4], BF16)
            words = grouped[:].rearrange("p c r t -> p c (r t)").bitcast(F32)
            interleave_words(engine, words[:, block(h, 2)], live["bank", ("f", g, j, h)])
            give_back("bank", ("f", g, j, h))

        def feature_quantize(g, j, h):
            src = live["fg", (g, j)][:, block(h, 2)].rearrange("p c r t -> p (c r t)")
            done = ("codes", ("f", g, j)) in live
            quantize(("f", g, j), "f%d" % j, K_PASS, E5M2, src, block(h, 2 * P))
            if done:
                give_back("fg", (g, j))

        def w_transpose(n, h):
            bank = take("bank", ("w", n, h), [P, 2, 2, P], F32)
            done = ("bank", ("w", n, 1 - h)) in live
            transpose_chunks(bank, live["w", n][:].bitcast(F32), h)
            if done:
                give_back("w", n)

        def w_evacuate(n, h, engine):
            words = w_grouped[h][:].rearrange("p c d t -> p c (d t)").bitcast(F32)
            interleave_words(engine, words[:, :, block(n, 2 * P)], live["bank", ("w", n, h)])
            give_back("bank", ("w", n, h))

        def w_quantize(c):
            src = w_grouped[c // 2][:].rearrange("p c d t -> p c (d t)")[:, c % 2]
            quantize(("w", c), "w%d" % c, D, E4M3, src, block(0, D))

        def interleave_rows(engine, dst, src):
            copy[engine](
                out=dst.rearrange("p (k i) j -> p k j i", i=4),
                in_=src.rearrange("p j (k i) -> p k j i", i=4),
            )

        def token_copy(g, c, engine):
            interleave_rows(engine, take("tg", (g, c), [P, K_PASS, 4], BF16)[:], dq[g][:, :, block(c, K_PASS)])

        def token_quantize(g, c):
            src = live["tg", (g, c)][:].rearrange("p k j -> p (k j)")
            quantize(("t", g, c), "t%d%d" % (g, c), K_PASS, E5M2, src, block(0, K_PASS))
            give_back("tg", (g, c))

        def x_copy(g, h, engine):
            interleave_rows(engine, take("xg", (g, h), [P, K_PASS, 4], BF16)[:], x_sb[g][:, :, block(h, K_PASS)])

        def x_quantize(g, h):
            src = live["xg", (g, h)][:].rearrange("p k j -> p (k j)")
            quantize(("x", g, h), "x%d%d" % (g, h), K_PASS, E4M3, src, block(0, K_PASS))
            give_back("xg", (g, h))

        def out_0_pass(g, j, n, c):
            acc = take("bank", ("o", g, j, n), [P, K_PASS], F32)
            multiply(acc[:], ("f", g, j), block(c, P), E5M2, ("w", c), block(n, K_PASS), E4M3, c == 0, c == CHUNKS - 1)

        def out_0_evacuate(g, j, n, engine):
            res = take("res", ("o", g, j), [P, 2, K_PASS], F32)
            copy[engine](out=res[:, n], in_=live["bank", ("o", g, j, n)][:])
            give_back("bank", ("o", g, j, n))

        def out_0_store(g, j):
            nc.sync.dma_start(out=out_0_rows[g][:, j, :], in_=live["res", ("o", g, j)][:].rearrange("p n k -> p (n k)"))
            give_back("res", ("o", g, j))

        def out_1_passes(c, d):
            acc = take("bank", ("p", c, d), [P, K_PASS], F32)
            for g in range(GROUPS):
                left = ("x", g, d // 4)
                multiply(acc[:], left, block(d % 4, P), E4M3, ("t", g, c), block(0, K_PASS), E5M2, g == 0, g == GROUPS - 1)

        def out_1_evacuate(c, d, engine):
            res = take("res", ("p", c, d // 2), [P, 2, K_PASS], F32)
            copy[engine](out=res[:, d % 2], in_=live["bank", ("p", c, d)][:])
            give_back("bank", ("p", c, d))

        def out_1_store(c, k):
            nc.sync.dma_start(out=out_1_rows[:, block(k, 2), block(c, K_PASS)], in_=live["res", ("p", c, k)][:])
            give_back("res", ("p", c, k))

        def out_1_store_half(c, d):
            nc.sync.dma_start(out=out_1_rows[:, d, block(c, K_PASS)], in_=live["res", ("p", c, d // 2)][:, d % 2])

        steps = {
            "tab": make_tables,
            "lg": load_g,
            "lw": load_w,
            "lx": load_x,
            "rs": rope_sin,
            "rc": rope_cos,
            "ra": rope_add,
            "ft": feature_transpose,
            "fe": feature_evacuate,
            "fq": feature_quantize,
            "tc": token_copy,
            "tq": token_quantize,
            "wt": w_transpose,
            "we": w_evacuate,
            "wq": w_quantize,
            "xc": x_copy,
            "xq": x_quantize,
            "om": out_0_pass,
            "oe": out_0_evacuate,
            "os": out_0_store,
            "pm": out_1_passes,
            "pe": out_1_evacuate,
            "ps": out_1_store,
            "ph": out_1_store_half,
        }
        with tc.manual_schedule():
            for line in ORDER:
                for step in line.split():
                    name, indices, engine = step.split(".")
                    arguments = [int(i) for i in indices] + ([engine] if engine else [])
                    steps[name](*arguments)
